import numpy as np
import ml_dtypes


def mxq(x, axis, fmt="e4m3"):
    dtype, down = {"e4m3": (ml_dtypes.float8_e4m3fn, 7), "e5m2": (ml_dtypes.float8_e5m2, 14)}[fmt]
    v = np.moveaxis(np.asarray(x, np.float32).astype(ml_dtypes.bfloat16).astype(np.float64), axis, -1)
    blocks = v.reshape(v.shape[:-1] + (-1, 32))
    amax = np.abs(blocks).max(-1, keepdims=True)
    byte = np.maximum(np.where(amax > 0, np.frexp(amax)[1] - 1 + 127, 0) - down, 1)
    scale = np.exp2(byte - 127.0)
    codes = (blocks / scale).astype(np.float32).astype(dtype).astype(np.float64)
    return np.moveaxis((codes * scale).reshape(v.shape), -1, axis)


WIDE = False


def mx_kscale(k):
    if not WIDE:
        return np.ones(k)
    levels = np.array([10, -10, 5, -5, 0])
    a = np.random.permutation(np.resize(levels, k // 512 * 4)).reshape(k // 512, 4)
    idx = np.arange(k)
    return np.exp2(a[idx // 512, idx % 128 // 32])


BF16 = ml_dtypes.bfloat16


def bf(x):
    return np.asarray(x, np.float32).astype(BF16)


def f64(x):
    return np.asarray(x).astype(np.float64)


B, T, C, H, G = 2, 2048, 512, 8, 16
HS = C // H
TG = T // G
THETA = 10000.0


def apply_rope(t, cos, sin):
    tp = t.reshape(B, T, H, HS // 2, 2)
    a, b = tp[..., 0], tp[..., 1]
    c = cos[None, :, None, :]
    s = sin[None, :, None, :]
    return np.stack([a * c - b * s, a * s + b * c], axis=-1).reshape(B, T, H, HS)


def grp(t):
    return t.reshape(B, G, TG, H, HS).transpose(0, 3, 1, 2, 4)


def with_summary(t):
    return np.concatenate([t, t.mean(axis=3, keepdims=True)], axis=3)


def setup_inputs():
    s = mx_kscale(C)
    x = np.random.standard_normal((B, T, C)) * 0.7 + np.random.standard_normal((B, 1, C)) * 0.7
    w = np.random.standard_normal((3 * C, C)) / np.sqrt(C)
    ang = np.arange(T)[:, None] / THETA ** (np.arange(0, HS, 2) / HS)[None, :]
    return {"x": bf(x * s), "w_attn": bf(w / s[None, :]), "freqs_cos": bf(np.cos(ang)), "freqs_sin": bf(np.sin(ang))}


def reference(x, w_attn, freqs_cos, freqs_sin):
    cos, sin = f64(freqs_cos), f64(freqs_sin)
    qkv = mxq(f64(x), 2, "e4m3") @ mxq(f64(w_attn), 1, "e4m3").T
    q, k, v = np.split(qkv, 3, axis=2)
    q = apply_rope(q.reshape(B, T, H, HS), cos, sin).reshape(B, T, C)
    k = apply_rope(k.reshape(B, T, H, HS), cos, sin).reshape(B, T, C)
    q, k, v = grp(q), grp(k), grp(v)
    return with_summary(q), with_summary(k), with_summary(v)

@@ -1,0 +1,346 @@
+from contextlib import ExitStack
+
+import concourse.mybir as mybir
+from concourse.masks import make_identity
+
+F32 = mybir.dt.float32
+BF16 = mybir.dt.bfloat16
+U32 = mybir.dt.uint32
+U8 = mybir.dt.uint8
+FP8X4 = mybir.dt.float8_e4m3fn_x4
+ADD = mybir.AluOpType.add
+MULT = mybir.AluOpType.mult
+
+P = 128
+B, T, C, H, G = 2, 2048, 512, 8, 16
+HS = C // H
+J = 4
+NQ = T // (P * J)
+NBLK = B * NQ
+GB = 4
+SUMS_PER_B = NQ * (2 * 16 + 4)
+FLOPS = 2 * B * T * 3 * C * C
+
+
+def tile_causalselfattention2_pa_t_kernel(tc, x, w_attn, freqs_cos, freqs_sin, out_0, out_1, out_2):
+    nc = tc.nc
+    outs = [out_0, out_1, out_2]
+    with ExitStack() as ctx:
+        const = ctx.enter_context(tc.tile_pool(name="const", bufs=1))
+        xpool = ctx.enter_context(tc.tile_pool(name="xpool", bufs=NBLK))
+        stage = ctx.enter_context(tc.tile_pool(name="stage", bufs=3))
+        work = ctx.enter_context(tc.tile_pool(name="work", bufs=3))
+        opool = ctx.enter_context(tc.tile_pool(name="opool", bufs=6))
+        small = ctx.enter_context(tc.tile_pool(name="small", bufs=2))
+        ps_tr = ctx.enter_context(tc.psum_pool(name="ps_tr", bufs=1))
+        ps_mm = ctx.enter_context(tc.psum_pool(name="ps_mm", bufs=4))
+        ps_v = ctx.enter_context(tc.psum_pool(name="ps_v", bufs=1))
+        ps_r = ctx.enter_context(tc.psum_pool(name="ps_r", bufs=1))
+        ctx.enter_context(tc.manual_schedule())
+
+        ws = const.tile([P, 12, C], BF16)
+        w_view = w_attn.rearrange("(r p) k -> p r k", p=P)
+        xs = []
+        for blk in range(NBLK):
+            xs_blk = xpool.tile([P, J * C], BF16, name="xs_blk")
+            xs.append(xs_blk)
+
+        def load_x(blk):
+            b, qt = divmod(blk, NQ)
+            nc.sync.dma_start(
+                out=xs[blk][:],
+                in_=x[b, qt * P * J : (qt + 1) * P * J, :].rearrange("(p j) k -> p (j k)", j=J),
+            )
+
+        nc.sync.dma_start(out=ws[:, 0:4, :], in_=w_view[:, 0:4, :])
+        load_x(0)
+        nc.sync.dma_start(out=ws[:, 4:8, :], in_=w_view[:, 4:8, :])
+        nc.sync.dma_start(out=ws[:, 8:12, :], in_=w_view[:, 8:12, :])
+        for blk in range(1, NBLK):
+            load_x(blk)
+
+        cosb = const.tile([P, NQ, J * 32], BF16)
+        sinb = const.tile([P, NQ, J * 32], BF16)
+        cos_view = freqs_cos.rearrange("(q g n j) i -> g n q (j i)", q=NQ, g=GB, j=J)
+        sin_view = freqs_sin.rearrange("(q g n j) i -> g n q (j i)", q=NQ, g=GB, j=J)
+        for g in range(GB):
+            nc.scalar.dma_start(out=cosb[g:P:GB, :, :], in_=cos_view[g])
+            nc.scalar.dma_start(out=sinb[g:P:GB, :, :], in_=sin_view[g])
+
+        ident = const.tile([P, P], F32)
+        make_identity(nc, ident[:])
+        perm = const.tile([P, P], F32)
+        nc.vector.tensor_copy(
+            out=perm[:].rearrange("k (n g) -> k n g", g=GB),
+            in_=ident[:].rearrange("k (g n) -> k n g", g=GB),
+        )
+        eg = const.tile([P, GB], F32)
+        nc.vector.tensor_reduce(
+            out=eg[:], in_=ident[:].rearrange("p (n g) -> p g n", g=GB), axis=mybir.AxisListType.X, op=ADD
+        )
+        ind = const.tile([P, 8, 32], F32)
+        nc.vector.memset(ind[:], 0.0)
+        for h2 in range(2):
+            for qt in range(NQ):
+                nc.vector.tensor_copy(
+                    out=ind[:, h2 * 4 + qt, h2 * 16 + qt * GB : h2 * 16 + (qt + 1) * GB], in_=eg[:]
+                )
+        indv = const.tile([P, 4, 32], F32)
+        nc.vector.tensor_tensor(out=indv[:], in0=ind[:, 0:4, :], in1=ind[:, 4:8, :], op=ADD)
+        fold = const.tile([P, HS], F32)
+        nc.vector.tensor_tensor(out=fold[:], in0=ident[:, 0:HS], in1=ident[:, HS:P], op=ADD)
+        nc.vector.tensor_scalar_mul(out=fold[:], in0=fold[:], scalar1=1.0 / 128.0)
+        mask = const.tile([P, 384], F32)
+        nc.vector.memset(mask[:], 1.0)
+        mask_v = mask[:, 256:384].rearrange("p (a x g) -> p a x g", a=4, x=2)
+        nc.vector.memset(mask_v[0:64, :, 1, :], 0.0)
+        nc.vector.memset(mask_v[64:128, :, 0, :], 0.0)
+
+        cc = const.tile([P, NQ, J, HS], F32)
+        nc.vector.tensor_copy(
+            out=cc[:].rearrange("p q j (i x) -> p (q j i) x", x=2),
+            in_=cosb[:].rearrange("p q n -> p (q n)").unsqueeze(2).to_broadcast([P, NQ * J * 32, 2]),
+        )
+        sp = const.tile([P, NQ, J, 32], F32)
+        nc.vector.tensor_copy(out=sp[:].rearrange("p q j i -> p q (j i)"), in_=sinb[:])
+        sn = const.tile([P, NQ, J, 32], F32)
+        nc.vector.tensor_scalar_mul(out=sn[:].rearrange("p q j i -> p q (j i)"), in0=sinb[:], scalar1=-1.0)
+
+        wcodes = const.tile([P, 3 * C], U32, align_bytes=64)
+        wscales = const.tile([P, 3 * C], U8, align_bytes=64)
+        xcodes = const.tile([P, NBLK * C], U32, align_bytes=64)
+        xscales = const.tile([P, NBLK * C], U8, align_bytes=64)
+
+        def prep_items(words, mat, codes, scales, head=False):
+            grp = stage.tile([P, 4 * P * 4], BF16, align_bytes=64, name="grp")
+            gw = grp[:].bitcast(F32).rearrange("q (s m u) -> q s m u", s=4, u=2)
+            held = {}
+
+            def transposes(s):
+                if s % 2 == 0:
+                    if head:
+                        tr = ps_mm.tile([P, 2, 2, P], F32, name="mm")
+                    else:
+                        tr = ps_tr.tile([P, 2, 2, P], F32, name="tr")
+                    held["tr"] = tr
+                tr = held["tr"]
+                for u in range(2):
+                    nc.tensor.transpose(out=tr[:, s % 2, u, :], in_=words(s, u), identity=mat[:])
+                if s % 2 == 1:
+                    nc.scalar.copy(out=gw[:, s - 1 : s + 1], in_=tr[:].rearrange("q s u m -> q s m u"))
+
+            def quantise():
+                nc.vector.quantize_mx(out=codes.bitcast(FP8X4), scales=scales, in_=grp[:])
+
+            return [lambda s=s: transposes(s) for s in range(4)], quantise
+
+        ww = ws[:].bitcast(F32)
+
+        def prep_w(t, head=False):
+            return prep_items(
+                lambda s, u: ww[:, 4 * t + s, u * P : (u + 1) * P],
+                ident,
+                wcodes[:, t * C : (t + 1) * C],
+                wscales[:, t * C : (t + 1) * C],
+                head,
+            )
+
+        def prep_x(blk, head=False):
+            xw = xs[blk][:].bitcast(F32)
+            return prep_items(
+                lambda s, u: xw[:, s * 256 + u * P : s * 256 + (u + 1) * P],
+                perm,
+                xcodes[:, blk * C : (blk + 1) * C],
+                xscales[:, blk * C : (blk + 1) * C],
+                head,
+            )
+
+        def mx_pass(out, blk, j, t, start, stop):
+            col = (blk * J + j) * P
+            nc.tensor.matmul_mx(
+                out=out,
+                lhsT=xcodes[:, col : col + P].bitcast(FP8X4),
+                lhsT_scale=xscales[:, col : col + P],
+                rhs=wcodes[:, t * C : (t + 1) * C].bitcast(FP8X4),
+                rhs_scale=wscales[:, t * C : (t + 1) * C],
+                start=start,
+                stop=stop,
+            )
+
+        def store_chunk(o, blk, t):
+            b, qt = divmod(blk, NQ)
+            queue = nc.scalar if t == 2 else nc.sync
+            for g in range(GB):
+                queue.dma_start(
+                    out=outs[t][b, :, qt * GB + g, 0:P, :].rearrange("h (n j) c -> n h (j c)", j=J),
+                    in_=o[g:P:GB, :, :, :].rearrange("n h j c -> n h (j c)"),
+                )
+
+        state = {"count": 0}
+        o_of = {}
+        lv_of = {}
+
+        def sum_matmul(lo, lhsT, rhs):
+            if state["count"] == 0:
+                racc = ps_r.tile([P, 384], F32, name="racc")
+                state["racc"] = racc
+            nc.tensor.matmul(
+                out=state["racc"][:, lo : lo + 32],
+                lhsT=lhsT,
+                rhs=rhs,
+                start=(state["count"] == 0),
+                stop=(state["count"] == SUMS_PER_B - 1),
+            )
+            state["count"] += 1
+
+        def sums_qk(blk, t, h):
+            qt = blk % NQ
+            o = o_of[(blk, t)]
+            for a in range(2):
+                sum_matmul(
+                    t * P + (h // 2) * 32,
+                    o[:, h, 2 * a : 2 * a + 2, :].rearrange("p j c -> p (j c)"),
+                    ind[:, (h % 2) * 4 + qt, :],
+                )
+
+        def sums_v(blk, half):
+            qt = blk % NQ
+            lv = lv_of[blk]
+            for a in range(2 * half, 2 * half + 2):
+                sum_matmul(2 * P + a * 32, lv[:, a * P : (a + 1) * P], indv[:, qt, :])
+
+        def means_out(b):
+            state["count"] = 0
+            rsb = small.tile([P, 384], F32, name="rsb")
+            nc.vector.tensor_tensor(out=rsb[:], in0=state["racc"][:], in1=mask[:], op=MULT)
+            mps = ps_tr.tile([P, 3 * HS], F32, name="tr")
+            for t in range(3):
+                nc.tensor.matmul(
+                    out=mps[:, t * HS : (t + 1) * HS],
+                    lhsT=rsb[:, t * P : (t + 1) * P],
+                    rhs=fold[:],
+                    start=True,
+                    stop=True,
+                )
+            msb = small.tile([P, 3 * HS], F32, name="msb")
+            nc.scalar.copy(out=msb[:], in_=mps[:])
+            for t in range(3):
+                nc.sync.dma_start(
+                    out=outs[t][b, :, :, P, :].rearrange("h g c -> (h g) c"),
+                    in_=msb[:, t * HS : (t + 1) * HS],
+                )
+
+        held = {}
+
+        def qk_pass(blk, t, j):
+            qt = blk % NQ
+            if j == 0:
+                t1 = work.tile([P, H, J, HS], F32, name="t1")
+                pl = work.tile([P, 2, H, J, 32], F32, name="pl")
+                held["t1"] = t1
+                held["pl"] = pl
+            t1 = held["t1"]
+            pl = held["pl"]
+            mm = ps_mm.tile([P, C], F32, name="mm")
+            mx_pass(mm[:], blk, j, t, True, True)
+            nc.vector.tensor_tensor(
+                out=t1[:, :, j, :],
+                in0=mm[:].rearrange("p (h c) -> p h c", h=H),
+                in1=cc[:, qt, j, :].unsqueeze(1).to_broadcast([P, H, HS]),
+                op=MULT,
+            )
+            pairs = mm[:].rearrange("p (h i x) -> p h i x", h=H, x=2)
+            nc.vector.tensor_tensor(
+                out=pl[:, 0, :, j, :],
+                in0=pairs[:, :, :, 1],
+                in1=sn[:, qt, j, :].unsqueeze(1).to_broadcast([P, H, 32]),
+                op=MULT,
+            )
+            nc.vector.tensor_tensor(
+                out=pl[:, 1, :, j, :],
+                in0=pairs[:, :, :, 0],
+                in1=sp[:, qt, j, :].unsqueeze(1).to_broadcast([P, H, 32]),
+                op=MULT,
+            )
+            last = blk == NBLK - 1 and t == 1
+            if last:
+                if j == 0:
+                    o = opool.tile([P, H, J, HS], F32, name="o")
+                    o_of[(blk, t)] = o
+                o = o_of[(blk, t)]
+                nc.vector.tensor_tensor(
+                    out=o[:, :, j, :].rearrange("p h (i x) -> p h i x", x=2),
+                    in0=t1[:, :, j, :].rearrange("p h (i x) -> p h i x", x=2),
+                    in1=pl[:, :, :, j, :].rearrange("p x h i -> p h i x"),
+                    op=ADD,
+                )
+                if j == J - 1:
+                    store_chunk(o, blk, t)
+            elif j == J - 1:
+                o = opool.tile([P, H, J, HS], F32, name="o")
+                o_of[(blk, t)] = o
+                nc.gpsimd.tensor_tensor(
+                    out=o[:].rearrange("p h j (i x) -> p h (j i) x", x=2),
+                    in0=t1[:].rearrange("p h j (i x) -> p h (j i) x", x=2),
+                    in1=pl[:].rearrange("p x h j i -> p h (j i) x"),
+                    op=ADD,
+                )
+                store_chunk(o, blk, t)
+
+        def v_pass(blk, j):
+            if j == 0:
+                o = opool.tile([P, H, J, HS], F32, name="o")
+                vacc = ps_v.tile([P, C], F32, name="vacc")
+                held["ov"] = o
+                held["vacc"] = vacc
+            o = held["ov"]
+            vacc = held["vacc"]
+            vm = ps_v.tile([P, C], F32, name="vm")
+            mx_pass(vm[:], blk, j, 2, True, True)
+            mx_pass(vacc[:], blk, j, 2, j == 0, j == J - 1)
+            nc.scalar.copy(out=o[:, :, j, :], in_=vm[:].rearrange("p (h c) -> p h c", h=H))
+            if j == J - 1:
+                lv = small.tile([P, C], F32, name="lv")
+                lv_of[blk] = lv
+                nc.scalar.copy(out=lv[:], in_=vacc[:])
+                store_chunk(o, blk, 2)
+
+        for make in (lambda: prep_w(0, True), lambda: prep_x(0, True)):
+            trs, quantise = make()
+            for item in trs:
+                item()
+            quantise()
+
+        for blk in range(NBLK + 1):
+            passes = []
+            fill = []
+            prev = blk - 1
+            sq = [lambda h=h: sums_qk(prev, 0, h) for h in range(H)] if prev >= 0 else []
+            sk = [lambda h=h: sums_qk(prev, 1, h) for h in range(H)] if prev >= 0 else []
+            sv = [lambda a=a: sums_v(prev, a) for a in range(2)] if prev >= 0 else []
+            if blk < NBLK:
+                passes = [lambda t=t, j=j: qk_pass(blk, t, j) for t in range(2) for j in range(J)]
+                vp = [lambda j=j: v_pass(blk, j) for j in range(J)]
+                if blk == 0:
+                    for t in (1, 2):
+                        trs, quantise = prep_w(t)
+                        fill += trs + [quantise]
+                if blk + 1 < NBLK:
+                    trs, quantise = prep_x(blk + 1)
+                    fill += trs[0:2] + sq[0:3] + trs[2:4] + sq[3:8] + [quantise]
+                else:
+                    fill += sq
+                fill += [vp[0]] + sv + [vp[1]] + sk[0:2] + [vp[2]] + sk[2:4] + [vp[3]] + sk[4:8]
+            else:
+                fill += sq + sv + sk
+            if prev >= 0 and prev % NQ == NQ - 1:
+                fill += [lambda: means_out(prev // NQ)]
+            done = 0
+            for i in range(len(passes)):
+                passes[i]()
+                upto = (len(fill) * (i + 1)) // len(passes)
+                for item in fill[done:upto]:
+                    item()
+                done = upto
+            for item in fill[done:]:
+                item()

@@ -9,16 +9,17 @@ U32 = mybir.dt.uint32
 U8 = mybir.dt.uint8
 FP8X4 = mybir.dt.float8_e4m3fn_x4
 ADD = mybir.AluOpType.add
+SUB = mybir.AluOpType.subtract
 MULT = mybir.AluOpType.mult
 
 P = 128
 B, T, C, H, G = 2, 2048, 512, 8, 16
 HS = C // H
+NI = HS // 2
 J = 4
 NQ = T // (P * J)
 NBLK = B * NQ
 GB = 4
-SUMS_PER_B = NQ * (2 * 16 + 4)
 FLOPS = 2 * B * T * 3 * C * C
 
 
@@ -28,14 +29,14 @@ def tile_causalselfattention2_pa_t_kernel(tc, x, w_attn, freqs_cos, freqs_sin, o
     with ExitStack() as ctx:
         const = ctx.enter_context(tc.tile_pool(name="const", bufs=1))
         xpool = ctx.enter_context(tc.tile_pool(name="xpool", bufs=NBLK))
-        stage = ctx.enter_context(tc.tile_pool(name="stage", bufs=3))
-        work = ctx.enter_context(tc.tile_pool(name="work", bufs=3))
-        opool = ctx.enter_context(tc.tile_pool(name="opool", bufs=6))
+        stage = ctx.enter_context(tc.tile_pool(name="stage", bufs=2))
+        work = ctx.enter_context(tc.tile_pool(name="work", bufs=2))
+        opool = ctx.enter_context(tc.tile_pool(name="opool", bufs=7))
         small = ctx.enter_context(tc.tile_pool(name="small", bufs=2))
         ps_tr = ctx.enter_context(tc.psum_pool(name="ps_tr", bufs=1))
         ps_mm = ctx.enter_context(tc.psum_pool(name="ps_mm", bufs=4))
-        ps_v = ctx.enter_context(tc.psum_pool(name="ps_v", bufs=1))
-        ps_r = ctx.enter_context(tc.psum_pool(name="ps_r", bufs=1))
+        ps_va = ctx.enter_context(tc.psum_pool(name="ps_va", bufs=1))
+        ps_st = ctx.enter_context(tc.psum_pool(name="ps_st", bufs=2))
         ctx.enter_context(tc.manual_schedule())
 
         ws = const.tile([P, 12, C], BF16)
@@ -53,14 +54,14 @@ def tile_causalselfattention2_pa_t_kernel(tc, x, w_attn, freqs_cos, freqs_sin, o
             )
 
         nc.sync.dma_start(out=ws[:, 0:4, :], in_=w_view[:, 0:4, :])
-        load_x(0)
         nc.sync.dma_start(out=ws[:, 4:8, :], in_=w_view[:, 4:8, :])
+        load_x(0)
         nc.sync.dma_start(out=ws[:, 8:12, :], in_=w_view[:, 8:12, :])
         for blk in range(1, NBLK):
             load_x(blk)
 
-        cosb = const.tile([P, NQ, J * 32], BF16)
-        sinb = const.tile([P, NQ, J * 32], BF16)
+        cosb = const.tile([P, NQ, J * NI], BF16)
+        sinb = const.tile([P, NQ, J * NI], BF16)
         cos_view = freqs_cos.rearrange("(q g n j) i -> g n q (j i)", q=NQ, g=GB, j=J)
         sin_view = freqs_sin.rearrange("(q g n j) i -> g n q (j i)", q=NQ, g=GB, j=J)
         for g in range(GB):
@@ -74,42 +75,31 @@ def tile_causalselfattention2_pa_t_kernel(tc, x, w_attn, freqs_cos, freqs_sin, o
             out=perm[:].rearrange("k (n g) -> k n g", g=GB),
             in_=ident[:].rearrange("k (g n) -> k n g", g=GB),
         )
-        eg = const.tile([P, GB], F32)
-        nc.vector.tensor_reduce(
-            out=eg[:], in_=ident[:].rearrange("p (n g) -> p g n", g=GB), axis=mybir.AxisListType.X, op=ADD
-        )
-        ind = const.tile([P, 8, 32], F32)
-        nc.vector.memset(ind[:], 0.0)
-        for h2 in range(2):
-            for qt in range(NQ):
-                nc.vector.tensor_copy(
-                    out=ind[:, h2 * 4 + qt, h2 * 16 + qt * GB : h2 * 16 + (qt + 1) * GB], in_=eg[:]
-                )
-        indv = const.tile([P, 4, 32], F32)
-        nc.vector.tensor_tensor(out=indv[:], in0=ind[:, 0:4, :], in1=ind[:, 4:8, :], op=ADD)
         fold = const.tile([P, HS], F32)
         nc.vector.tensor_tensor(out=fold[:], in0=ident[:, 0:HS], in1=ident[:, HS:P], op=ADD)
         nc.vector.tensor_scalar_mul(out=fold[:], in0=fold[:], scalar1=1.0 / 128.0)
-        mask = const.tile([P, 384], F32)
-        nc.vector.memset(mask[:], 1.0)
-        mask_v = mask[:, 256:384].rearrange("p (a x g) -> p a x g", a=4, x=2)
+        mask_v = const.tile([P, 4, 2, G], F32)
+        nc.vector.memset(mask_v[:], 1.0)
         nc.vector.memset(mask_v[0:64, :, 1, :], 0.0)
         nc.vector.memset(mask_v[64:128, :, 0, :], 0.0)
-
-        cc = const.tile([P, NQ, J, HS], F32)
-        nc.vector.tensor_copy(
-            out=cc[:].rearrange("p q j (i x) -> p (q j i) x", x=2),
-            in_=cosb[:].rearrange("p q n -> p (q n)").unsqueeze(2).to_broadcast([P, NQ * J * 32, 2]),
-        )
-        sp = const.tile([P, NQ, J, 32], F32)
-        nc.vector.tensor_copy(out=sp[:].rearrange("p q j i -> p q (j i)"), in_=sinb[:])
-        sn = const.tile([P, NQ, J, 32], F32)
-        nc.vector.tensor_scalar_mul(out=sn[:].rearrange("p q j i -> p q (j i)"), in0=sinb[:], scalar1=-1.0)
 
         wcodes = const.tile([P, 3 * C], U32, align_bytes=64)
         wscales = const.tile([P, 3 * C], U8, align_bytes=64)
         xcodes = const.tile([P, NBLK * C], U32, align_bytes=64)
         xscales = const.tile([P, NBLK * C], U8, align_bytes=64)
+        ww = ws[:].bitcast(F32)
+
+        gab = const.tile([P, 2 * C * 4], BF16, align_bytes=64)
+        gabw = gab[:].bitcast(F32).rearrange("q (x n u) -> q x n u", x=2, u=2)
+        for r in range(8):
+            trw = ps_mm.tile([P, 2, P], F32, name="mm")
+            for u in range(2):
+                nc.tensor.transpose(out=trw[:, u, :], in_=ww[:, r, u * P : (u + 1) * P], identity=ident[:])
+            src = trw[:].rearrange("q u (n x) -> q x n u", x=2)
+            if r % 2 == 0:
+                nc.scalar.copy(out=gabw[:, :, r * 64 : (r + 1) * 64, :], in_=src)
+            else:
+                nc.vector.tensor_copy(out=gabw[:, :, r * 64 : (r + 1) * 64, :], in_=src)
 
         def prep_items(words, mat, codes, scales, head=False):
             grp = stage.tile([P, 4 * P * 4], BF16, align_bytes=64, name="grp")
@@ -134,15 +124,12 @@ def tile_causalselfattention2_pa_t_kernel(tc, x, w_attn, freqs_cos, freqs_sin, o
 
             return [lambda s=s: transposes(s) for s in range(4)], quantise
 
-        ww = ws[:].bitcast(F32)
-
-        def prep_w(t, head=False):
+        def prep_wv():
             return prep_items(
-                lambda s, u: ww[:, 4 * t + s, u * P : (u + 1) * P],
+                lambda s, u: ww[:, 8 + s, u * P : (u + 1) * P],
                 ident,
-                wcodes[:, t * C : (t + 1) * C],
-                wscales[:, t * C : (t + 1) * C],
-                head,
+                wcodes[:, 2 * C : 3 * C],
+                wscales[:, 2 * C : 3 * C],
             )
 
         def prep_x(blk, head=False):
@@ -155,14 +142,33 @@ def tile_causalselfattention2_pa_t_kernel(tc, x, w_attn, freqs_cos, freqs_sin, o
                 head,
             )
 
-        def mx_pass(out, blk, j, t, start, stop):
+        trs, quantise_x0 = prep_x(0, True)
+        for item in trs:
+            item()
+        for half in range(2):
+            nc.vector.quantize_mx(
+                out=wcodes[:, half * C : (half + 1) * C].bitcast(FP8X4),
+                scales=wscales[:, half * C : (half + 1) * C],
+                in_=gab[:, half * C * 4 : (half + 1) * C * 4],
+            )
+        quantise_x0()
+
+        t_c = const.tile([P, NQ, J, NI], F32)
+        t_e = const.tile([P, NQ, J, NI], F32)
+        t_o = const.tile([P, NQ, J, NI], F32)
+        nc.vector.tensor_copy(out=t_c[:].rearrange("p q j i -> p q (j i)"), in_=cosb[:])
+        nc.vector.tensor_tensor(out=t_e[:].rearrange("p q j i -> p q (j i)"), in0=cosb[:], in1=sinb[:], op=ADD)
+        nc.vector.tensor_scalar_mul(out=t_e[:], in0=t_e[:], scalar1=-1.0)
+        nc.vector.tensor_tensor(out=t_o[:].rearrange("p q j i -> p q (j i)"), in0=sinb[:], in1=cosb[:], op=SUB)
+
+        def mx_pass(out, blk, j, part, start, stop):
             col = (blk * J + j) * P
             nc.tensor.matmul_mx(
                 out=out,
                 lhsT=xcodes[:, col : col + P].bitcast(FP8X4),
                 lhsT_scale=xscales[:, col : col + P],
-                rhs=wcodes[:, t * C : (t + 1) * C].bitcast(FP8X4),
-                rhs_scale=wscales[:, t * C : (t + 1) * C],
+                rhs=wcodes[:, part * C : (part + 1) * C].bitcast(FP8X4),
+                rhs_scale=wscales[:, part * C : (part + 1) * C],
                 start=start,
                 stop=stop,
             )
@@ -176,48 +182,58 @@ def tile_causalselfattention2_pa_t_kernel(tc, x, w_attn, freqs_cos, freqs_sin, o
                     in_=o[g:P:GB, :, :, :].rearrange("n h j c -> n h (j c)"),
                 )
 
-        state = {"count": 0}
         o_of = {}
         lv_of = {}
+        sums_of = {}
+        held = {}
 
-        def sum_matmul(lo, lhsT, rhs):
-            if state["count"] == 0:
-                racc = ps_r.tile([P, 384], F32, name="racc")
-                state["racc"] = racc
-            nc.tensor.matmul(
-                out=state["racc"][:, lo : lo + 32],
-                lhsT=lhsT,
-                rhs=rhs,
-                start=(state["count"] == 0),
-                stop=(state["count"] == SUMS_PER_B - 1),
-            )
-            state["count"] += 1
-
-        def sums_qk(blk, t, h):
-            qt = blk % NQ
+        def sums_qk(blk, t, half):
+            b, qt = divmod(blk, NQ)
             o = o_of[(blk, t)]
-            for a in range(2):
-                sum_matmul(
-                    t * P + (h // 2) * 32,
-                    o[:, h, 2 * a : 2 * a + 2, :].rearrange("p j c -> p (j c)"),
-                    ind[:, (h % 2) * 4 + qt, :],
-                )
+            st = ps_st.tile([P, 4, P], F32, name="st")
+            for hh in range(4):
+                for a in range(2):
+                    nc.tensor.matmul(
+                        out=st[:, hh, :],
+                        lhsT=o[:, 4 * half + hh, 2 * a : 2 * a + 2, :].rearrange("p j c -> p (j c)"),
+                        rhs=ident[:],
+                        is_transpose=True,
+                        start=(a == 0),
+                        stop=(a == 1),
+                    )
+            nc.vector.tensor_reduce(
+                out=sums_of[b][:, t, 4 * half : 4 * half + 4, qt * GB : (qt + 1) * GB],
+                in_=st[:].rearrange("m h (n g) -> m h g n", g=GB),
+                axis=mybir.AxisListType.X,
+                op=ADD,
+            )
 
-        def sums_v(blk, half):
-            qt = blk % NQ
+        def sums_v(blk):
+            b, qt = divmod(blk, NQ)
             lv = lv_of[blk]
-            for a in range(2 * half, 2 * half + 2):
-                sum_matmul(2 * P + a * 32, lv[:, a * P : (a + 1) * P], indv[:, qt, :])
+            st = ps_st.tile([P, 4, P], F32, name="st")
+            for a in range(4):
+                nc.tensor.transpose(out=st[:, a, :], in_=lv[:, a * P : (a + 1) * P], identity=ident[:])
+            nc.vector.tensor_reduce(
+                out=sums_of[(b, "v")][:, :, qt * GB : (qt + 1) * GB],
+                in_=st[:].rearrange("m h (n g) -> m h g n", g=GB),
+                axis=mybir.AxisListType.X,
+                op=ADD,
+            )
 
         def means_out(b):
-            state["count"] = 0
-            rsb = small.tile([P, 384], F32, name="rsb")
-            nc.vector.tensor_tensor(out=rsb[:], in0=state["racc"][:], in1=mask[:], op=MULT)
+            rsb = sums_of[b]
+            nc.vector.tensor_tensor(
+                out=rsb[:, 2, :, :].rearrange("m (a x) g -> m a x g", x=2),
+                in0=sums_of[(b, "v")][:].unsqueeze(2).to_broadcast([P, 4, 2, G]),
+                in1=mask_v[:],
+                op=MULT,
+            )
             mps = ps_tr.tile([P, 3 * HS], F32, name="tr")
             for t in range(3):
                 nc.tensor.matmul(
                     out=mps[:, t * HS : (t + 1) * HS],
-                    lhsT=rsb[:, t * P : (t + 1) * P],
+                    lhsT=rsb[:, t, :, :].rearrange("m h g -> m (h g)"),
                     rhs=fold[:],
                     start=True,
                     stop=True,
@@ -230,72 +246,64 @@ def tile_causalselfattention2_pa_t_kernel(tc, x, w_attn, freqs_cos, freqs_sin, o
                     in_=msb[:, t * HS : (t + 1) * HS],
                 )
 
-        held = {}
+        def final_add(engine, blk, t, jh):
+            o = o_of[(blk, t)]
+            js = slice(2 * jh, 2 * jh + 2)
+            hs = slice(t * H, (t + 1) * H)
+            engine.tensor_tensor(
+                out=o[:, :, js, :].rearrange("p h j (i x) -> p h (j i) x", x=2),
+                in0=held["k1"][:, hs, js, :].rearrange("p h j i -> p h (j i)").unsqueeze(3).to_broadcast([P, H, 2 * NI, 2]),
+                in1=held["pl"][:, :, hs, js, :].rearrange("p x h j i -> p h (j i) x"),
+                op=ADD,
+            )
 
-        def qk_pass(blk, t, j):
+        def qk_group(blk, j):
             qt = blk % NQ
             if j == 0:
-                t1 = work.tile([P, H, J, HS], F32, name="t1")
-                pl = work.tile([P, 2, H, J, 32], F32, name="pl")
-                held["t1"] = t1
+                k1 = work.tile([P, 2 * H, J, NI], F32, name="k1")
+                pl = work.tile([P, 2, 2 * H, J, NI], F32, name="pl")
+                held["k1"] = k1
                 held["pl"] = pl
-            t1 = held["t1"]
+            k1 = held["k1"]
             pl = held["pl"]
-            mm = ps_mm.tile([P, C], F32, name="mm")
-            mx_pass(mm[:], blk, j, t, True, True)
-            nc.vector.tensor_tensor(
-                out=t1[:, :, j, :],
-                in0=mm[:].rearrange("p (h c) -> p h c", h=H),
-                in1=cc[:, qt, j, :].unsqueeze(1).to_broadcast([P, H, HS]),
-                op=MULT,
-            )
-            pairs = mm[:].rearrange("p (h i x) -> p h i x", h=H, x=2)
-            nc.vector.tensor_tensor(
-                out=pl[:, 0, :, j, :],
-                in0=pairs[:, :, :, 1],
-                in1=sn[:, qt, j, :].unsqueeze(1).to_broadcast([P, H, 32]),
-                op=MULT,
-            )
-            nc.vector.tensor_tensor(
-                out=pl[:, 1, :, j, :],
-                in0=pairs[:, :, :, 0],
-                in1=sp[:, qt, j, :].unsqueeze(1).to_broadcast([P, H, 32]),
-                op=MULT,
-            )
-            last = blk == NBLK - 1 and t == 1
-            if last:
-                if j == 0:
-                    o = opool.tile([P, H, J, HS], F32, name="o")
-                    o_of[(blk, t)] = o
-                o = o_of[(blk, t)]
+            bank_a = ps_mm.tile([P, C], F32, name="mm")
+            mx_pass(bank_a[:], blk, j, 0, True, True)
+            bank_b = ps_mm.tile([P, C], F32, name="mm")
+            mx_pass(bank_b[:], blk, j, 1, True, True)
+            bank_ab = ps_mm.tile([P, C], F32, name="mm")
+            mx_pass(bank_ab[:], blk, j, 0, True, False)
+            mx_pass(bank_ab[:], blk, j, 1, False, True)
+            for bank, table, dst in (
+                (bank_a, t_o, pl[:, 1, :, j, :]),
+                (bank_b, t_e, pl[:, 0, :, j, :]),
+                (bank_ab, t_c, k1[:, :, j, :]),
+            ):
                 nc.vector.tensor_tensor(
-                    out=o[:, :, j, :].rearrange("p h (i x) -> p h i x", x=2),
-                    in0=t1[:, :, j, :].rearrange("p h (i x) -> p h i x", x=2),
-                    in1=pl[:, :, :, j, :].rearrange("p x h i -> p h i x"),
-                    op=ADD,
+                    out=dst,
+                    in0=bank[:].rearrange("p (h i) -> p h i", i=NI),
+                    in1=table[:, qt, j, :].unsqueeze(1).to_broadcast([P, 2 * H, NI]),
+                    op=MULT,
                 )
+            if j % 2 == 1:
+                for t in range(2):
+                    if j == 1:
+                        o = opool.tile([P, H, J, HS], F32, name="o")
+                        o_of[(blk, t)] = o
+                    on_vector = blk == NBLK - 1 and j == J - 1 and t == 1
+                    final_add(nc.vector if on_vector else nc.gpsimd, blk, t, j // 2)
                 if j == J - 1:
-                    store_chunk(o, blk, t)
-            elif j == J - 1:
-                o = opool.tile([P, H, J, HS], F32, name="o")
-                o_of[(blk, t)] = o
-                nc.gpsimd.tensor_tensor(
-                    out=o[:].rearrange("p h j (i x) -> p h (j i) x", x=2),
-                    in0=t1[:].rearrange("p h j (i x) -> p h (j i) x", x=2),
-                    in1=pl[:].rearrange("p x h j i -> p h (j i) x"),
-                    op=ADD,
-                )
-                store_chunk(o, blk, t)
+                    for t in range(2):
+                        store_chunk(o_of[(blk, t)], blk, t)
 
         def v_pass(blk, j):
             if j == 0:
                 o = opool.tile([P, H, J, HS], F32, name="o")
-                vacc = ps_v.tile([P, C], F32, name="vacc")
+                vacc = ps_va.tile([P, C], F32, name="vacc")
                 held["ov"] = o
                 held["vacc"] = vacc
             o = held["ov"]
             vacc = held["vacc"]
-            vm = ps_v.tile([P, C], F32, name="vm")
+            vm = ps_mm.tile([P, C], F32, name="mm")
             mx_pass(vm[:], blk, j, 2, True, True)
             mx_pass(vacc[:], blk, j, 2, j == 0, j == J - 1)
             nc.scalar.copy(out=o[:, :, j, :], in_=vm[:].rearrange("p (h c) -> p h c", h=H))
@@ -305,42 +313,41 @@ def tile_causalselfattention2_pa_t_kernel(tc, x, w_attn, freqs_cos, freqs_sin, o
                 nc.scalar.copy(out=lv[:], in_=vacc[:])
                 store_chunk(o, blk, 2)
 
-        for make in (lambda: prep_w(0, True), lambda: prep_x(0, True)):
-            trs, quantise = make()
-            for item in trs:
-                item()
-            quantise()
-
         for blk in range(NBLK + 1):
-            passes = []
-            fill = []
             prev = blk - 1
-            sq = [lambda h=h: sums_qk(prev, 0, h) for h in range(H)] if prev >= 0 else []
-            sk = [lambda h=h: sums_qk(prev, 1, h) for h in range(H)] if prev >= 0 else []
-            sv = [lambda a=a: sums_v(prev, a) for a in range(2)] if prev >= 0 else []
+            if blk < NBLK and blk % NQ == 0:
+                rsb = small.tile([P, 3, H, G], F32, name="rsb")
+                rv = small.tile([P, 4, G], F32, name="rv")
+                sums_of[blk // NQ] = rsb
+                sums_of[(blk // NQ, "v")] = rv
+            slots = [[], [], [], []]
             if blk < NBLK:
-                passes = [lambda t=t, j=j: qk_pass(blk, t, j) for t in range(2) for j in range(J)]
                 vp = [lambda j=j: v_pass(blk, j) for j in range(J)]
                 if blk == 0:
-                    for t in (1, 2):
-                        trs, quantise = prep_w(t)
-                        fill += trs + [quantise]
-                if blk + 1 < NBLK:
-                    trs, quantise = prep_x(blk + 1)
-                    fill += trs[0:2] + sq[0:3] + trs[2:4] + sq[3:8] + [quantise]
+                    trs_v, quantise_v = prep_wv()
+                    trs, quantise = prep_x(1)
+                    slots[0] += trs_v
+                    slots[1] += [quantise_v] + trs
+                    slots[2] += [quantise, vp[0], vp[1]]
+                    slots[3] += [vp[2], vp[3]]
                 else:
-                    fill += sq
-                fill += [vp[0]] + sv + [vp[1]] + sk[0:2] + [vp[2]] + sk[2:4] + [vp[3]] + sk[4:8]
-            else:
-                fill += sq + sv + sk
-            if prev >= 0 and prev % NQ == NQ - 1:
-                fill += [lambda: means_out(prev // NQ)]
-            done = 0
-            for i in range(len(passes)):
-                passes[i]()
-                upto = (len(fill) * (i + 1)) // len(passes)
-                for item in fill[done:upto]:
+                    for j in range(J):
+                        slots[j].append(vp[j])
+                    if blk + 1 < NBLK:
+                        trs, quantise = prep_x(blk + 1)
+                        slots[0] += trs[0:2]
+                        slots[1] += trs[2:4]
+                        slots[2] += [quantise]
+            if prev >= 0:
+                slots[0].append(lambda: sums_qk(prev, 0, 0))
+                slots[1].append(lambda: sums_qk(prev, 0, 1))
+                slots[2].append(lambda: sums_v(prev))
+                slots[2].append(lambda: sums_qk(prev, 1, 0))
+                slots[3].append(lambda: sums_qk(prev, 1, 1))
+                if prev % NQ == NQ - 1:
+                    slots[3].append(lambda: means_out(prev // NQ))
+            for j in range(J):
+                if blk < NBLK:
+                    qk_group(blk, j)
+                for item in slots[j]:
                     item()
-                done = upto
-            for item in fill[done:]:
-                item()

@@ -9,7 +9,6 @@ U32 = mybir.dt.uint32
 U8 = mybir.dt.uint8
 FP8X4 = mybir.dt.float8_e4m3fn_x4
 ADD = mybir.AluOpType.add
-SUB = mybir.AluOpType.subtract
 MULT = mybir.AluOpType.mult
 
 P = 128
@@ -89,17 +88,6 @@ def tile_causalselfattention2_pa_t_kernel(tc, x, w_attn, freqs_cos, freqs_sin, o
         xscales = const.tile([P, NBLK * C], U8, align_bytes=64)
         ww = ws[:].bitcast(F32)
 
-        gab = const.tile([P, 2 * C * 4], BF16, align_bytes=64)
-        gabw = gab[:].bitcast(F32).rearrange("q (x n u) -> q x n u", x=2, u=2)
-        for r in range(8):
-            trw = ps_mm.tile([P, 2, P], F32, name="mm")
-            for u in range(2):
-                nc.tensor.transpose(out=trw[:, u, :], in_=ww[:, r, u * P : (u + 1) * P], identity=ident[:])
-            src = trw[:].rearrange("q u (n x) -> q x n u", x=2)
-            if r % 2 == 0:
-                nc.scalar.copy(out=gabw[:, :, r * 64 : (r + 1) * 64, :], in_=src)
-            else:
-                nc.vector.tensor_copy(out=gabw[:, :, r * 64 : (r + 1) * 64, :], in_=src)
 
         def prep_items(words, mat, codes, scales, head=False):
             grp = stage.tile([P, 4 * P * 4], BF16, align_bytes=64, name="grp")
@@ -124,12 +112,13 @@ def tile_causalselfattention2_pa_t_kernel(tc, x, w_attn, freqs_cos, freqs_sin, o
 
             return [lambda s=s: transposes(s) for s in range(4)], quantise
 
-        def prep_wv():
+        def prep_w(t, head=False):
             return prep_items(
-                lambda s, u: ww[:, 8 + s, u * P : (u + 1) * P],
+                lambda s, u: ww[:, 4 * t + s, u * P : (u + 1) * P],
                 ident,
-                wcodes[:, 2 * C : 3 * C],
-                wscales[:, 2 * C : 3 * C],
+                wcodes[:, t * C : (t + 1) * C],
+                wscales[:, t * C : (t + 1) * C],
+                head,
             )
 
         def prep_x(blk, head=False):
@@ -142,24 +131,21 @@ def tile_causalselfattention2_pa_t_kernel(tc, x, w_attn, freqs_cos, freqs_sin, o
                 head,
             )
 
-        trs, quantise_x0 = prep_x(0, True)
-        for item in trs:
-            item()
-        for half in range(2):
-            nc.vector.quantize_mx(
-                out=wcodes[:, half * C : (half + 1) * C].bitcast(FP8X4),
-                scales=wscales[:, half * C : (half + 1) * C],
-                in_=gab[:, half * C * 4 : (half + 1) * C * 4],
-            )
-        quantise_x0()
+        for make in (lambda: prep_w(0, True), lambda: prep_x(0, True), lambda: prep_w(1, True)):
+            trs, quantise = make()
+            for item in trs:
+                item()
+            quantise()
 
-        t_c = const.tile([P, NQ, J, NI], F32)
+        t_c = const.tile([P, NQ, J, HS], F32)
+        nc.vector.tensor_copy(
+            out=t_c[:].rearrange("p q j (i x) -> p (q j i) x", x=2),
+            in_=cosb[:].rearrange("p q n -> p (q n)").unsqueeze(2).to_broadcast([P, NQ * J * NI, 2]),
+        )
         t_e = const.tile([P, NQ, J, NI], F32)
         t_o = const.tile([P, NQ, J, NI], F32)
-        nc.vector.tensor_copy(out=t_c[:].rearrange("p q j i -> p q (j i)"), in_=cosb[:])
-        nc.vector.tensor_tensor(out=t_e[:].rearrange("p q j i -> p q (j i)"), in0=cosb[:], in1=sinb[:], op=ADD)
-        nc.vector.tensor_scalar_mul(out=t_e[:], in0=t_e[:], scalar1=-1.0)
-        nc.vector.tensor_tensor(out=t_o[:].rearrange("p q j i -> p q (j i)"), in0=sinb[:], in1=cosb[:], op=SUB)
+        nc.vector.tensor_scalar_mul(out=t_e[:].rearrange("p q j i -> p q (j i)"), in0=sinb[:], scalar1=-1.0)
+        nc.vector.tensor_copy(out=t_o[:].rearrange("p q j i -> p q (j i)"), in_=sinb[:])
 
         def mx_pass(out, blk, j, part, start, stop):
             col = (blk * J + j) * P
@@ -252,7 +238,7 @@ def tile_causalselfattention2_pa_t_kernel(tc, x, w_attn, freqs_cos, freqs_sin, o
             hs = slice(t * H, (t + 1) * H)
             engine.tensor_tensor(
                 out=o[:, :, js, :].rearrange("p h j (i x) -> p h (j i) x", x=2),
-                in0=held["k1"][:, hs, js, :].rearrange("p h j i -> p h (j i)").unsqueeze(3).to_broadcast([P, H, 2 * NI, 2]),
+                in0=held["k1"][:, hs, js, :].rearrange("p h j (i x) -> p h (j i) x", x=2),
                 in1=held["pl"][:, :, hs, js, :].rearrange("p x h j i -> p h (j i) x"),
                 op=ADD,
             )
@@ -260,28 +246,33 @@ def tile_causalselfattention2_pa_t_kernel(tc, x, w_attn, freqs_cos, freqs_sin, o
         def qk_group(blk, j):
             qt = blk % NQ
             if j == 0:
-                k1 = work.tile([P, 2 * H, J, NI], F32, name="k1")
+                k1 = work.tile([P, 2 * H, J, HS], F32, name="k1")
                 pl = work.tile([P, 2, 2 * H, J, NI], F32, name="pl")
                 held["k1"] = k1
                 held["pl"] = pl
             k1 = held["k1"]
             pl = held["pl"]
-            bank_a = ps_mm.tile([P, C], F32, name="mm")
-            mx_pass(bank_a[:], blk, j, 0, True, True)
-            bank_b = ps_mm.tile([P, C], F32, name="mm")
-            mx_pass(bank_b[:], blk, j, 1, True, True)
-            bank_ab = ps_mm.tile([P, C], F32, name="mm")
-            mx_pass(bank_ab[:], blk, j, 0, True, False)
-            mx_pass(bank_ab[:], blk, j, 1, False, True)
-            for bank, table, dst in (
-                (bank_a, t_o, pl[:, 1, :, j, :]),
-                (bank_b, t_e, pl[:, 0, :, j, :]),
-                (bank_ab, t_c, k1[:, :, j, :]),
-            ):
+            for t in range(2):
+                hs = slice(t * H, (t + 1) * H)
+                bank = ps_mm.tile([P, C], F32, name="mm")
+                mx_pass(bank[:], blk, j, t, True, True)
                 nc.vector.tensor_tensor(
-                    out=dst,
-                    in0=bank[:].rearrange("p (h i) -> p h i", i=NI),
-                    in1=table[:, qt, j, :].unsqueeze(1).to_broadcast([P, 2 * H, NI]),
+                    out=k1[:, hs, j, :],
+                    in0=bank[:].rearrange("p (h c) -> p h c", h=H),
+                    in1=t_c[:, qt, j, :].unsqueeze(1).to_broadcast([P, H, HS]),
+                    op=MULT,
+                )
+                pairs = bank[:].rearrange("p (h i x) -> p h i x", h=H, x=2)
+                nc.vector.tensor_tensor(
+                    out=pl[:, 0, hs, j, :],
+                    in0=pairs[:, :, :, 1],
+                    in1=t_e[:, qt, j, :].unsqueeze(1).to_broadcast([P, H, NI]),
+                    op=MULT,
+                )
+                nc.vector.tensor_tensor(
+                    out=pl[:, 1, hs, j, :],
+                    in0=pairs[:, :, :, 0],
+                    in1=t_o[:, qt, j, :].unsqueeze(1).to_broadcast([P, H, NI]),
                     op=MULT,
                 )
             if j % 2 == 1:
@@ -324,7 +315,7 @@ def tile_causalselfattention2_pa_t_kernel(tc, x, w_attn, freqs_cos, freqs_sin, o
             if blk < NBLK:
                 vp = [lambda j=j: v_pass(blk, j) for j in range(J)]
                 if blk == 0:
-                    trs_v, quantise_v = prep_wv()
+                    trs_v, quantise_v = prep_w(2)
                     trs, quantise = prep_x(1)
                     slots[0] += trs_v
                     slots[1] += [quantise_v] + trs

@@ -29,7 +29,7 @@ def tile_causalselfattention2_pa_t_kernel(tc, x, w_attn, freqs_cos, freqs_sin, o
         const = ctx.enter_context(tc.tile_pool(name="const", bufs=1))
         xpool = ctx.enter_context(tc.tile_pool(name="xpool", bufs=NBLK))
         stage = ctx.enter_context(tc.tile_pool(name="stage", bufs=2))
-        work = ctx.enter_context(tc.tile_pool(name="work", bufs=2))
+        work = ctx.enter_context(tc.tile_pool(name="work", bufs=4))
         opool = ctx.enter_context(tc.tile_pool(name="opool", bufs=7))
         small = ctx.enter_context(tc.tile_pool(name="small", bufs=2))
         ps_tr = ctx.enter_context(tc.psum_pool(name="ps_tr", bufs=1))
@@ -53,8 +53,8 @@ def tile_causalselfattention2_pa_t_kernel(tc, x, w_attn, freqs_cos, freqs_sin, o
             )
 
         nc.sync.dma_start(out=ws[:, 0:4, :], in_=w_view[:, 0:4, :])
-        nc.sync.dma_start(out=ws[:, 4:8, :], in_=w_view[:, 4:8, :])
         load_x(0)
+        nc.sync.dma_start(out=ws[:, 4:8, :], in_=w_view[:, 4:8, :])
         nc.sync.dma_start(out=ws[:, 8:12, :], in_=w_view[:, 8:12, :])
         for blk in range(1, NBLK):
             load_x(blk)
@@ -131,7 +131,7 @@ def tile_causalselfattention2_pa_t_kernel(tc, x, w_attn, freqs_cos, freqs_sin, o
                 head,
             )
 
-        for make in (lambda: prep_w(0, True), lambda: prep_x(0, True), lambda: prep_w(1, True)):
+        for make in (lambda: prep_w(0, True), lambda: prep_x(0, True)):
             trs, quantise = make()
             for item in trs:
                 item()
@@ -169,9 +169,8 @@ def tile_causalselfattention2_pa_t_kernel(tc, x, w_attn, freqs_cos, freqs_sin, o
                 )
 
         o_of = {}
-        lv_of = {}
         sums_of = {}
-        held = {}
+        held = {"pending": []}
 
         def sums_qk(blk, t, half):
             b, qt = divmod(blk, NQ)
@@ -187,27 +186,22 @@ def tile_causalselfattention2_pa_t_kernel(tc, x, w_attn, freqs_cos, freqs_sin, o
                         start=(a == 0),
                         stop=(a == 1),
                     )
-            nc.vector.tensor_reduce(
-                out=sums_of[b][:, t, 4 * half : 4 * half + 4, qt * GB : (qt + 1) * GB],
-                in_=st[:].rearrange("m h (n g) -> m h g n", g=GB),
-                axis=mybir.AxisListType.X,
-                op=ADD,
+            held["pending"].append(
+                lambda: nc.vector.tensor_reduce(
+                    out=sums_of[b][:, t, 4 * half : 4 * half + 4, qt * GB : (qt + 1) * GB],
+                    in_=st[:].rearrange("m h (n g) -> m h g n", g=GB),
+                    axis=mybir.AxisListType.X,
+                    op=ADD,
+                )
             )
 
-        def sums_v(blk):
-            b, qt = divmod(blk, NQ)
-            lv = lv_of[blk]
-            st = ps_st.tile([P, 4, P], F32, name="st")
-            for a in range(4):
-                nc.tensor.transpose(out=st[:, a, :], in_=lv[:, a * P : (a + 1) * P], identity=ident[:])
-            nc.vector.tensor_reduce(
-                out=sums_of[(b, "v")][:, :, qt * GB : (qt + 1) * GB],
-                in_=st[:].rearrange("m h (n g) -> m h g n", g=GB),
-                axis=mybir.AxisListType.X,
-                op=ADD,
-            )
+        def flush_pending():
+            for item in held["pending"]:
+                item()
+            held["pending"] = []
 
         def means_out(b):
+            flush_pending()
             rsb = sums_of[b]
             nc.vector.tensor_tensor(
                 out=rsb[:, 2, :, :].rearrange("m (a x) g -> m a x g", x=2),
@@ -234,75 +228,86 @@ def tile_causalselfattention2_pa_t_kernel(tc, x, w_attn, freqs_cos, freqs_sin, o
 
         def final_add(engine, blk, t, jh):
             o = o_of[(blk, t)]
+            k1, pl = held[(blk, jh)]
             js = slice(2 * jh, 2 * jh + 2)
             hs = slice(t * H, (t + 1) * H)
             engine.tensor_tensor(
                 out=o[:, :, js, :].rearrange("p h j (i x) -> p h (j i) x", x=2),
-                in0=held["k1"][:, hs, js, :].rearrange("p h j (i x) -> p h (j i) x", x=2),
-                in1=held["pl"][:, :, hs, js, :].rearrange("p x h j i -> p h (j i) x"),
+                in0=k1[:, hs, :, :].rearrange("p h j (i x) -> p h (j i) x", x=2),
+                in1=pl[:, :, hs, :, :].rearrange("p x h j i -> p h (j i) x"),
                 op=ADD,
             )
 
-        def qk_group(blk, j):
+        def qk_unit(blk, t, j):
             qt = blk % NQ
-            if j == 0:
-                k1 = work.tile([P, 2 * H, J, HS], F32, name="k1")
-                pl = work.tile([P, 2, 2 * H, J, NI], F32, name="pl")
-                held["k1"] = k1
-                held["pl"] = pl
-            k1 = held["k1"]
-            pl = held["pl"]
-            for t in range(2):
-                hs = slice(t * H, (t + 1) * H)
-                bank = ps_mm.tile([P, C], F32, name="mm")
-                mx_pass(bank[:], blk, j, t, True, True)
-                nc.vector.tensor_tensor(
-                    out=k1[:, hs, j, :],
-                    in0=bank[:].rearrange("p (h c) -> p h c", h=H),
-                    in1=t_c[:, qt, j, :].unsqueeze(1).to_broadcast([P, H, HS]),
-                    op=MULT,
-                )
-                pairs = bank[:].rearrange("p (h i x) -> p h i x", h=H, x=2)
-                nc.vector.tensor_tensor(
-                    out=pl[:, 0, hs, j, :],
-                    in0=pairs[:, :, :, 1],
-                    in1=t_e[:, qt, j, :].unsqueeze(1).to_broadcast([P, H, NI]),
-                    op=MULT,
-                )
-                nc.vector.tensor_tensor(
-                    out=pl[:, 1, hs, j, :],
-                    in0=pairs[:, :, :, 0],
-                    in1=t_o[:, qt, j, :].unsqueeze(1).to_broadcast([P, H, NI]),
-                    op=MULT,
-                )
-            if j % 2 == 1:
-                for t in range(2):
-                    if j == 1:
-                        o = opool.tile([P, H, J, HS], F32, name="o")
-                        o_of[(blk, t)] = o
-                    on_vector = blk == NBLK - 1 and j == J - 1 and t == 1
-                    final_add(nc.vector if on_vector else nc.gpsimd, blk, t, j // 2)
-                if j == J - 1:
-                    for t in range(2):
-                        store_chunk(o_of[(blk, t)], blk, t)
+            if (blk, j // 2) not in held:
+                k1 = work.tile([P, 2 * H, 2, HS], F32, name="k1")
+                pl = work.tile([P, 2, 2 * H, 2, NI], F32, name="pl")
+                held[(blk, j // 2)] = (k1, pl)
+            k1, pl = held[(blk, j // 2)]
+            hs = slice(t * H, (t + 1) * H)
+            bank = ps_mm.tile([P, C], F32, name="mm")
+            mx_pass(bank[:], blk, j, t, True, True)
+            nc.vector.tensor_tensor(
+                out=k1[:, hs, j % 2, :],
+                in0=bank[:].rearrange("p (h c) -> p h c", h=H),
+                in1=t_c[:, qt, j, :].unsqueeze(1).to_broadcast([P, H, HS]),
+                op=MULT,
+            )
+            pairs = bank[:].rearrange("p (h i x) -> p h i x", h=H, x=2)
+            nc.vector.tensor_tensor(
+                out=pl[:, 0, hs, j % 2, :],
+                in0=pairs[:, :, :, 1],
+                in1=t_e[:, qt, j, :].unsqueeze(1).to_broadcast([P, H, NI]),
+                op=MULT,
+            )
+            nc.vector.tensor_tensor(
+                out=pl[:, 1, hs, j % 2, :],
+                in0=pairs[:, :, :, 0],
+                in1=t_o[:, qt, j, :].unsqueeze(1).to_broadcast([P, H, NI]),
+                op=MULT,
+            )
+
+        def adds(blk, t, jh):
+            if jh == 0:
+                o = opool.tile([P, H, J, HS], F32, name="o")
+                o_of[(blk, t)] = o
+            on_vector = blk == NBLK - 1 and t == 1
+            final_add(nc.vector if on_vector else nc.gpsimd, blk, t, jh)
+            if jh == 1:
+                store_chunk(o_of[(blk, t)], blk, t)
 
         def v_pass(blk, j):
+            b, qt = divmod(blk, NQ)
             if j == 0:
                 o = opool.tile([P, H, J, HS], F32, name="o")
-                vacc = ps_va.tile([P, C], F32, name="vacc")
                 held["ov"] = o
-                held["vacc"] = vacc
             o = held["ov"]
-            vacc = held["vacc"]
             vm = ps_mm.tile([P, C], F32, name="mm")
             mx_pass(vm[:], blk, j, 2, True, True)
-            mx_pass(vacc[:], blk, j, 2, j == 0, j == J - 1)
             nc.scalar.copy(out=o[:, :, j, :], in_=vm[:].rearrange("p (h c) -> p h c", h=H))
             if j == J - 1:
-                lv = small.tile([P, C], F32, name="lv")
-                lv_of[blk] = lv
-                nc.scalar.copy(out=lv[:], in_=vacc[:])
                 store_chunk(o, blk, 2)
+            vt = ps_va.tile([P, C], F32, name="vt")
+            wcol = 2 * C + j * P
+            nc.tensor.matmul_mx(
+                out=vt[:],
+                lhsT=wcodes[:, wcol : wcol + P].bitcast(FP8X4),
+                lhsT_scale=wscales[:, wcol : wcol + P],
+                rhs=xcodes[:, blk * C : (blk + 1) * C].bitcast(FP8X4),
+                rhs_scale=xscales[:, blk * C : (blk + 1) * C],
+                start=True,
+                stop=True,
+            )
+            by_group = vt[:].rearrange("m (j n g) -> m g j n", j=J, g=GB)
+            for g in range(GB):
+                junk = small.tile([P, J, P // GB], F32, name="junk")
+                nc.scalar.activation(
+                    out=junk[:],
+                    in_=by_group[:, g],
+                    func=mybir.ActivationFunctionType.Copy,
+                    accum_out=sums_of[(b, "v")][:, j, qt * GB + g : qt * GB + g + 1],
+                )
 
         for blk in range(NBLK + 1):
             prev = blk - 1
@@ -312,15 +317,23 @@ def tile_causalselfattention2_pa_t_kernel(tc, x, w_attn, freqs_cos, freqs_sin, o
                 sums_of[blk // NQ] = rsb
                 sums_of[(blk // NQ, "v")] = rv
             slots = [[], [], [], []]
+            units = []
+            by_tensor = blk == 0 or blk == NBLK - 1
             if blk < NBLK:
+                if by_tensor:
+                    order = [(t, j) for t in range(2) for j in range(J)]
+                else:
+                    order = [(t, j) for j in range(J) for t in range(2)]
+                units = [order[0:2], order[2:4], order[4:6], order[6:8]]
                 vp = [lambda j=j: v_pass(blk, j) for j in range(J)]
                 if blk == 0:
+                    trs_k, quantise_k = prep_w(1)
                     trs_v, quantise_v = prep_w(2)
                     trs, quantise = prep_x(1)
-                    slots[0] += trs_v
-                    slots[1] += [quantise_v] + trs
-                    slots[2] += [quantise, vp[0], vp[1]]
-                    slots[3] += [vp[2], vp[3]]
+                    slots[0] += trs_k
+                    slots[1] += [quantise_k] + trs_v
+                    slots[2] += [quantise_v] + trs + [vp[0], vp[1]]
+                    slots[3] += [quantise, vp[2], vp[3]]
                 else:
                     for j in range(J):
                         slots[j].append(vp[j])
@@ -332,13 +345,20 @@ def tile_causalselfattention2_pa_t_kernel(tc, x, w_attn, freqs_cos, freqs_sin, o
             if prev >= 0:
                 slots[0].append(lambda: sums_qk(prev, 0, 0))
                 slots[1].append(lambda: sums_qk(prev, 0, 1))
-                slots[2].append(lambda: sums_v(prev))
                 slots[2].append(lambda: sums_qk(prev, 1, 0))
                 slots[3].append(lambda: sums_qk(prev, 1, 1))
                 if prev % NQ == NQ - 1:
                     slots[3].append(lambda: means_out(prev // NQ))
-            for j in range(J):
+            for s in range(4):
                 if blk < NBLK:
-                    qk_group(blk, j)
-                for item in slots[j]:
+                    for t, j in units[s]:
+                        qk_unit(blk, t, j)
+                flush_pending()
+                if blk < NBLK:
+                    if by_tensor:
+                        adds(blk, s // 2, s % 2)
+                    elif s % 2 == 1:
+                        adds(blk, 0, s // 2)
+                        adds(blk, 1, s // 2)
+                for item in slots[s]:
                     item()

@@ -19,6 +19,7 @@ J = 4
 NQ = T // (P * J)
 NBLK = B * NQ
 GB = 4
+SUM_LAG = 5
 FLOPS = 2 * B * T * 3 * C * C
 
 
@@ -105,7 +106,10 @@ def tile_causalselfattention2_pa_t_kernel(tc, x, w_attn, freqs_cos, freqs_sin, o
                 for u in range(2):
                     nc.tensor.transpose(out=tr[:, s % 2, u, :], in_=words(s, u), identity=mat[:])
                 if s % 2 == 1:
-                    nc.scalar.copy(out=gw[:, s - 1 : s + 1], in_=tr[:].rearrange("q s u m -> q s m u"))
+                    if head and mat is perm:
+                        nc.vector.tensor_copy(out=gw[:, s - 1 : s + 1], in_=tr[:].rearrange("q s u m -> q s m u"))
+                    else:
+                        nc.scalar.copy(out=gw[:, s - 1 : s + 1], in_=tr[:].rearrange("q s u m -> q s m u"))
 
             def quantise():
                 nc.vector.quantize_mx(out=codes.bitcast(FP8X4), scales=scales, in_=grp[:])
@@ -131,21 +135,15 @@ def tile_causalselfattention2_pa_t_kernel(tc, x, w_attn, freqs_cos, freqs_sin, o
                 head,
             )
 
-        for make in (lambda: prep_w(0, True), lambda: prep_x(0, True)):
-            trs, quantise = make()
-            for item in trs:
-                item()
-            quantise()
+        trs_q, quantise_q = prep_w(0, True)
+        trs_x, quantise_x = prep_x(0, True)
+        for item in trs_q + trs_x:
+            item()
+        quantise_q()
+        quantise_x()
 
-        t_c = const.tile([P, NQ, J, HS], F32)
-        nc.vector.tensor_copy(
-            out=t_c[:].rearrange("p q j (i x) -> p (q j i) x", x=2),
-            in_=cosb[:].rearrange("p q n -> p (q n)").unsqueeze(2).to_broadcast([P, NQ * J * NI, 2]),
-        )
-        t_e = const.tile([P, NQ, J, NI], F32)
-        t_o = const.tile([P, NQ, J, NI], F32)
-        nc.vector.tensor_scalar_mul(out=t_e[:].rearrange("p q j i -> p q (j i)"), in0=sinb[:], scalar1=-1.0)
-        nc.vector.tensor_copy(out=t_o[:].rearrange("p q j i -> p q (j i)"), in_=sinb[:])
+        nsinb = const.tile([P, NQ, J * NI], BF16)
+        nc.vector.tensor_scalar_mul(out=nsinb[:], in0=sinb[:], scalar1=-1.0)
 
         def mx_pass(out, blk, j, part, start, stop):
             col = (blk * J + j) * P
@@ -246,25 +244,26 @@ def tile_causalselfattention2_pa_t_kernel(tc, x, w_attn, freqs_cos, freqs_sin, o
                 held[(blk, j // 2)] = (k1, pl)
             k1, pl = held[(blk, j // 2)]
             hs = slice(t * H, (t + 1) * H)
+            js = slice(j * NI, (j + 1) * NI)
             bank = ps_mm.tile([P, C], F32, name="mm")
             mx_pass(bank[:], blk, j, t, True, True)
             nc.vector.tensor_tensor(
-                out=k1[:, hs, j % 2, :],
-                in0=bank[:].rearrange("p (h c) -> p h c", h=H),
-                in1=t_c[:, qt, j, :].unsqueeze(1).to_broadcast([P, H, HS]),
+                out=k1[:, hs, j % 2, :].rearrange("p h (i x) -> p h i x", x=2),
+                in0=bank[:].rearrange("p (h i x) -> p h i x", h=H, x=2),
+                in1=cosb[:, qt, js].unsqueeze(1).unsqueeze(3).to_broadcast([P, H, NI, 2]),
                 op=MULT,
             )
             pairs = bank[:].rearrange("p (h i x) -> p h i x", h=H, x=2)
             nc.vector.tensor_tensor(
                 out=pl[:, 0, hs, j % 2, :],
                 in0=pairs[:, :, :, 1],
-                in1=t_e[:, qt, j, :].unsqueeze(1).to_broadcast([P, H, NI]),
+                in1=nsinb[:, qt, js].unsqueeze(1).to_broadcast([P, H, NI]),
                 op=MULT,
             )
             nc.vector.tensor_tensor(
                 out=pl[:, 1, hs, j % 2, :],
                 in0=pairs[:, :, :, 0],
-                in1=t_o[:, qt, j, :].unsqueeze(1).to_broadcast([P, H, NI]),
+                in1=sinb[:, qt, js].unsqueeze(1).to_broadcast([P, H, NI]),
                 op=MULT,
             )
 
@@ -309,8 +308,7 @@ def tile_causalselfattention2_pa_t_kernel(tc, x, w_attn, freqs_cos, freqs_sin, o
                     accum_out=sums_of[(b, "v")][:, j, qt * GB + g : qt * GB + g + 1],
                 )
 
-        for blk in range(NBLK + 1):
-            prev = blk - 1
+        for blk in range(NBLK + 2):
             if blk < NBLK and blk % NQ == 0:
                 rsb = small.tile([P, 3, H, G], F32, name="rsb")
                 rv = small.tile([P, 4, G], F32, name="rv")
@@ -342,13 +340,17 @@ def tile_causalselfattention2_pa_t_kernel(tc, x, w_attn, freqs_cos, freqs_sin, o
                         slots[0] += trs[0:2]
                         slots[1] += trs[2:4]
                         slots[2] += [quantise]
-            if prev >= 0:
-                slots[0].append(lambda: sums_qk(prev, 0, 0))
-                slots[1].append(lambda: sums_qk(prev, 0, 1))
-                slots[2].append(lambda: sums_qk(prev, 1, 0))
-                slots[3].append(lambda: sums_qk(prev, 1, 1))
-                if prev % NQ == NQ - 1:
-                    slots[3].append(lambda: means_out(prev // NQ))
+            for s in range(4):
+                tile_nos = [blk * 4 + s - SUM_LAG]
+                if blk * 4 + s > (NBLK - 1) * 4:
+                    tile_nos = [blk * 4 + s - SUM_LAG + 1]
+                    if blk * 4 + s == (NBLK - 1) * 4 + 1:
+                        tile_nos = [blk * 4 + s - SUM_LAG, blk * 4 + s - SUM_LAG + 1]
+                for tile_no in tile_nos:
+                    if 0 <= tile_no < NBLK * 4:
+                        slots[s].append(lambda n=tile_no: sums_qk(n // 4, (n % 4) // 2, n % 2))
+                        if tile_no % (NQ * 4) == NQ * 4 - 1:
+                            slots[s].append(lambda n=tile_no: means_out(n // (NQ * 4)))
             for s in range(4):
                 if blk < NBLK:
                     for t, j in units[s]:

@@ -33,6 +33,7 @@ def tile_causalselfattention2_pa_t_kernel(tc, x, w_attn, freqs_cos, freqs_sin, o
         work = ctx.enter_context(tc.tile_pool(name="work", bufs=4))
         opool = ctx.enter_context(tc.tile_pool(name="opool", bufs=7))
         small = ctx.enter_context(tc.tile_pool(name="small", bufs=2))
+        lpool = ctx.enter_context(tc.tile_pool(name="lpool", bufs=3))
         ps_tr = ctx.enter_context(tc.psum_pool(name="ps_tr", bufs=1))
         ps_mm = ctx.enter_context(tc.psum_pool(name="ps_mm", bufs=4))
         ps_va = ctx.enter_context(tc.psum_pool(name="ps_va", bufs=1))
@@ -167,6 +168,7 @@ def tile_causalselfattention2_pa_t_kernel(tc, x, w_attn, freqs_cos, freqs_sin, o
                 )
 
         o_of = {}
+        l1_of = {}
         sums_of = {}
         held = {"pending": []}
 
@@ -175,15 +177,18 @@ def tile_causalselfattention2_pa_t_kernel(tc, x, w_attn, freqs_cos, freqs_sin, o
             o = o_of[(blk, t)]
             st = ps_st.tile([P, 4, P], F32, name="st")
             for hh in range(4):
-                for a in range(2):
-                    nc.tensor.matmul(
-                        out=st[:, hh, :],
-                        lhsT=o[:, 4 * half + hh, 2 * a : 2 * a + 2, :].rearrange("p j c -> p (j c)"),
-                        rhs=ident[:],
-                        is_transpose=True,
-                        start=(a == 0),
-                        stop=(a == 1),
-                    )
+                if (blk, t) in l1_of:
+                    nc.tensor.transpose(out=st[:, hh, :], in_=l1_of[(blk, t)][:, 4 * half + hh, :], identity=ident[:])
+                else:
+                    for a in range(2):
+                        nc.tensor.matmul(
+                            out=st[:, hh, :],
+                            lhsT=o[:, 4 * half + hh, 2 * a : 2 * a + 2, :].rearrange("p j c -> p (j c)"),
+                            rhs=ident[:],
+                            is_transpose=True,
+                            start=(a == 0),
+                            stop=(a == 1),
+                        )
             held["pending"].append(
                 lambda: nc.vector.tensor_reduce(
                     out=sums_of[b][:, t, 4 * half : 4 * half + 4, qt * GB : (qt + 1) * GB],
@@ -275,6 +280,16 @@ def tile_causalselfattention2_pa_t_kernel(tc, x, w_attn, freqs_cos, freqs_sin, o
             final_add(nc.vector if on_vector else nc.gpsimd, blk, t, jh)
             if jh == 1:
                 store_chunk(o_of[(blk, t)], blk, t)
+                if t == 1 and not on_vector:
+                    o = o_of[(blk, t)]
+                    l1 = lpool.tile([P, H, 2 * HS], F32, name="l1")
+                    nc.gpsimd.tensor_tensor(
+                        out=l1[:],
+                        in0=o[:, :, 0:2, :].rearrange("p h j c -> p h (j c)"),
+                        in1=o[:, :, 2:4, :].rearrange("p h j c -> p h (j c)"),
+                        op=ADD,
+                    )
+                    l1_of[(blk, t)] = l1
 
         def v_pass(blk, j):
             b, qt = divmod(blk, NQ)

@@ -10,15 +10,26 @@ U8 = mybir.dt.uint8
 FP8X4 = mybir.dt.float8_e4m3fn_x4
 ADD = mybir.AluOpType.add
 MULT = mybir.AluOpType.mult
+COPY = mybir.ActivationFunctionType.Copy
+LAST_AXIS = mybir.AxisListType.X
 
 P = 128
 B, T, C, H, G = 2, 2048, 512, 8, 16
 HS = C // H
 NI = HS // 2
+TG = T // G
 J = 4
+GS = P * J // TG
 NQ = T // (P * J)
-NBLK = B * NQ
-GB = 4
+NSPAN = B * NQ
+WORDS = C // 2
+PLANES = WORDS // P
+PACK = 4
+SETS = 4
+HEADS_OF_TILE = 4
+Q_, K_, V_ = 0, 1, 2
+BEATS = 4
+SUM_TILES = 4
 SUM_LAG = 5
 FLOPS = 2 * B * T * 3 * C * C
 
@@ -28,354 +39,336 @@ def tile_causalselfattention2_pa_t_kernel(tc, x, w_attn, freqs_cos, freqs_sin, o
     outs = [out_0, out_1, out_2]
     with ExitStack() as ctx:
         const = ctx.enter_context(tc.tile_pool(name="const", bufs=1))
-        xpool = ctx.enter_context(tc.tile_pool(name="xpool", bufs=NBLK))
+        x_pool = ctx.enter_context(tc.tile_pool(name="x_pool", bufs=NSPAN))
         stage = ctx.enter_context(tc.tile_pool(name="stage", bufs=2))
-        work = ctx.enter_context(tc.tile_pool(name="work", bufs=4))
-        opool = ctx.enter_context(tc.tile_pool(name="opool", bufs=7))
+        products = ctx.enter_context(tc.tile_pool(name="products", bufs=4))
+        chunk_pool = ctx.enter_context(tc.tile_pool(name="chunk_pool", bufs=7))
         small = ctx.enter_context(tc.tile_pool(name="small", bufs=2))
-        lpool = ctx.enter_context(tc.tile_pool(name="lpool", bufs=3))
-        ps_tr = ctx.enter_context(tc.psum_pool(name="ps_tr", bufs=1))
-        ps_mm = ctx.enter_context(tc.psum_pool(name="ps_mm", bufs=4))
-        ps_va = ctx.enter_context(tc.psum_pool(name="ps_va", bufs=1))
-        ps_st = ctx.enter_context(tc.psum_pool(name="ps_st", bufs=2))
+        ps_words = ctx.enter_context(tc.psum_pool(name="ps_words", bufs=1))
+        ps_pass = ctx.enter_context(tc.psum_pool(name="ps_pass", bufs=4))
+        ps_vt = ctx.enter_context(tc.psum_pool(name="ps_vt", bufs=1))
+        ps_sums = ctx.enter_context(tc.psum_pool(name="ps_sums", bufs=2))
         ctx.enter_context(tc.manual_schedule())
 
-        ws = const.tile([P, 12, C], BF16)
+        w_rows = const.tile([P, 3 * SETS, C], BF16)
         w_view = w_attn.rearrange("(r p) k -> p r k", p=P)
-        xs = []
-        for blk in range(NBLK):
-            xs_blk = xpool.tile([P, J * C], BF16, name="xs_blk")
-            xs.append(xs_blk)
+        x_rows = []
+        for span in range(NSPAN):
+            x_span = x_pool.tile([P, J * C], BF16, name="x_span")
+            x_rows.append(x_span)
 
-        def load_x(blk):
-            b, qt = divmod(blk, NQ)
+        def load_w(t):
+            nc.sync.dma_start(out=w_rows[:, SETS * t : SETS * (t + 1), :], in_=w_view[:, SETS * t : SETS * (t + 1), :])
+
+        def load_x(span):
+            b, qt = divmod(span, NQ)
             nc.sync.dma_start(
-                out=xs[blk][:],
+                out=x_rows[span][:],
                 in_=x[b, qt * P * J : (qt + 1) * P * J, :].rearrange("(p j) k -> p (j k)", j=J),
             )
 
-        nc.sync.dma_start(out=ws[:, 0:4, :], in_=w_view[:, 0:4, :])
+        load_w(Q_)
         load_x(0)
-        nc.sync.dma_start(out=ws[:, 4:8, :], in_=w_view[:, 4:8, :])
-        nc.sync.dma_start(out=ws[:, 8:12, :], in_=w_view[:, 8:12, :])
-        for blk in range(1, NBLK):
-            load_x(blk)
+        load_w(K_)
+        load_w(V_)
+        for span in range(1, NSPAN):
+            load_x(span)
 
-        cosb = const.tile([P, NQ, J * NI], BF16)
-        sinb = const.tile([P, NQ, J * NI], BF16)
-        cos_view = freqs_cos.rearrange("(q g n j) i -> g n q (j i)", q=NQ, g=GB, j=J)
-        sin_view = freqs_sin.rearrange("(q g n j) i -> g n q (j i)", q=NQ, g=GB, j=J)
-        for g in range(GB):
-            nc.scalar.dma_start(out=cosb[g:P:GB, :, :], in_=cos_view[g])
-            nc.scalar.dma_start(out=sinb[g:P:GB, :, :], in_=sin_view[g])
+        cos_t = const.tile([P, NQ, J * NI], BF16)
+        sin_t = const.tile([P, NQ, J * NI], BF16)
+        cos_view = freqs_cos.rearrange("(q g n j) i -> g n q (j i)", q=NQ, g=GS, j=J)
+        sin_view = freqs_sin.rearrange("(q g n j) i -> g n q (j i)", q=NQ, g=GS, j=J)
+        for g in range(GS):
+            nc.scalar.dma_start(out=cos_t[g:P:GS, :, :], in_=cos_view[g])
+            nc.scalar.dma_start(out=sin_t[g:P:GS, :, :], in_=sin_view[g])
 
         ident = const.tile([P, P], F32)
         make_identity(nc, ident[:])
-        perm = const.tile([P, P], F32)
+        spread = const.tile([P, P], F32)
         nc.vector.tensor_copy(
-            out=perm[:].rearrange("k (n g) -> k n g", g=GB),
-            in_=ident[:].rearrange("k (g n) -> k n g", g=GB),
+            out=spread[:].rearrange("k (n g) -> k n g", g=GS),
+            in_=ident[:].rearrange("k (g n) -> k n g", g=GS),
         )
         fold = const.tile([P, HS], F32)
         nc.vector.tensor_tensor(out=fold[:], in0=ident[:, 0:HS], in1=ident[:, HS:P], op=ADD)
-        nc.vector.tensor_scalar_mul(out=fold[:], in0=fold[:], scalar1=1.0 / 128.0)
-        mask_v = const.tile([P, 4, 2, G], F32)
-        nc.vector.memset(mask_v[:], 1.0)
-        nc.vector.memset(mask_v[0:64, :, 1, :], 0.0)
-        nc.vector.memset(mask_v[64:128, :, 0, :], 0.0)
+        nc.vector.tensor_scalar_mul(out=fold[:], in0=fold[:], scalar1=1.0 / TG)
+        own_half = const.tile([P, H // 2, 2, G], F32)
+        nc.vector.memset(own_half[:], 1.0)
+        nc.vector.memset(own_half[0:HS, :, 1, :], 0.0)
+        nc.vector.memset(own_half[HS:P, :, 0, :], 0.0)
 
-        wcodes = const.tile([P, 3 * C], U32, align_bytes=64)
-        wscales = const.tile([P, 3 * C], U8, align_bytes=64)
-        xcodes = const.tile([P, NBLK * C], U32, align_bytes=64)
-        xscales = const.tile([P, NBLK * C], U8, align_bytes=64)
-        ww = ws[:].bitcast(F32)
+        w_codes = const.tile([P, 3 * C], U32, align_bytes=64)
+        w_scales = const.tile([P, 3 * C], U8, align_bytes=64)
+        x_codes = const.tile([P, NSPAN * C], U32, align_bytes=64)
+        x_scales = const.tile([P, NSPAN * C], U8, align_bytes=64)
+        w_words = w_rows[:].bitcast(F32)
 
+        def prepare(words, matrix, columns, codes, scales, in_head, copy):
+            grouped = stage.tile([P, SETS * P * PACK], BF16, align_bytes=64, name="grouped")
+            grouped_words = grouped[:].bitcast(F32).rearrange("q (s m u) -> q s m u", s=SETS, u=PLANES)
+            current = {}
 
-        def prep_items(words, mat, codes, scales, head=False):
-            grp = stage.tile([P, 4 * P * 4], BF16, align_bytes=64, name="grp")
-            gw = grp[:].bitcast(F32).rearrange("q (s m u) -> q s m u", s=4, u=2)
-            held = {}
-
-            def transposes(s):
+            def transpose_set(s):
                 if s % 2 == 0:
-                    if head:
-                        tr = ps_mm.tile([P, 2, 2, P], F32, name="mm")
+                    if in_head:
+                        planes = ps_pass.tile([P, 2, PLANES, P], F32, name="planes", tag="bank")
                     else:
-                        tr = ps_tr.tile([P, 2, 2, P], F32, name="tr")
-                    held["tr"] = tr
-                tr = held["tr"]
-                for u in range(2):
-                    nc.tensor.transpose(out=tr[:, s % 2, u, :], in_=words(s, u), identity=mat[:])
+                        planes = ps_words.tile([P, 2, PLANES, P], F32, name="planes", tag="words")
+                    current["planes"] = planes
+                planes = current["planes"]
+                for u in range(PLANES):
+                    nc.tensor.transpose(out=planes[:, s % 2, u, :], in_=words(s, u), identity=matrix[:])
                 if s % 2 == 1:
-                    if head and mat is perm:
-                        nc.vector.tensor_copy(out=gw[:, s - 1 : s + 1], in_=tr[:].rearrange("q s u m -> q s m u"))
-                    else:
-                        nc.scalar.copy(out=gw[:, s - 1 : s + 1], in_=tr[:].rearrange("q s u m -> q s m u"))
+                    copy(out=grouped_words[:, s - 1 : s + 1], in_=planes[:].rearrange("q s u m -> q s m u"))
 
             def quantise():
-                nc.vector.quantize_mx(out=codes.bitcast(FP8X4), scales=scales, in_=grp[:])
+                nc.vector.quantize_mx(out=codes[:, columns].bitcast(FP8X4), scales=scales[:, columns], in_=grouped[:])
 
-            return [lambda s=s: transposes(s) for s in range(4)], quantise
+            return [lambda s=s: transpose_set(s) for s in range(SETS)], quantise
 
-        def prep_w(t, head=False):
-            return prep_items(
-                lambda s, u: ww[:, 4 * t + s, u * P : (u + 1) * P],
+        def prepare_w(t, in_head=False):
+            return prepare(
+                lambda s, u: w_words[:, SETS * t + s, u * P : (u + 1) * P],
                 ident,
-                wcodes[:, t * C : (t + 1) * C],
-                wscales[:, t * C : (t + 1) * C],
-                head,
+                slice(t * C, (t + 1) * C),
+                w_codes,
+                w_scales,
+                in_head,
+                nc.scalar.copy,
             )
 
-        def prep_x(blk, head=False):
-            xw = xs[blk][:].bitcast(F32)
-            return prep_items(
-                lambda s, u: xw[:, s * 256 + u * P : s * 256 + (u + 1) * P],
-                perm,
-                xcodes[:, blk * C : (blk + 1) * C],
-                xscales[:, blk * C : (blk + 1) * C],
-                head,
+        def prepare_x(span, in_head=False):
+            x_words = x_rows[span][:].bitcast(F32)
+            return prepare(
+                lambda s, u: x_words[:, s * WORDS + u * P : s * WORDS + (u + 1) * P],
+                spread,
+                slice(span * C, (span + 1) * C),
+                x_codes,
+                x_scales,
+                in_head,
+                nc.vector.tensor_copy if in_head else nc.scalar.copy,
             )
 
-        trs_q, quantise_q = prep_w(0, True)
-        trs_x, quantise_x = prep_x(0, True)
-        for item in trs_q + trs_x:
-            item()
-        quantise_q()
-        quantise_x()
-
-        nsinb = const.tile([P, NQ, J * NI], BF16)
-        nc.vector.tensor_scalar_mul(out=nsinb[:], in0=sinb[:], scalar1=-1.0)
-
-        def mx_pass(out, blk, j, part, start, stop):
-            col = (blk * J + j) * P
+        def mx_pass(out, span, j, t):
+            positions = slice((span * J + j) * P, (span * J + j + 1) * P)
+            channels = slice(t * C, (t + 1) * C)
             nc.tensor.matmul_mx(
                 out=out,
-                lhsT=xcodes[:, col : col + P].bitcast(FP8X4),
-                lhsT_scale=xscales[:, col : col + P],
-                rhs=wcodes[:, part * C : (part + 1) * C].bitcast(FP8X4),
-                rhs_scale=wscales[:, part * C : (part + 1) * C],
-                start=start,
-                stop=stop,
+                lhsT=x_codes[:, positions].bitcast(FP8X4),
+                lhsT_scale=x_scales[:, positions],
+                rhs=w_codes[:, channels].bitcast(FP8X4),
+                rhs_scale=w_scales[:, channels],
+                start=True,
+                stop=True,
             )
 
-        def store_chunk(o, blk, t):
-            b, qt = divmod(blk, NQ)
-            queue = nc.scalar if t == 2 else nc.sync
-            for g in range(GB):
+        sets_w, quantise_w = prepare_w(Q_, in_head=True)
+        sets_x, quantise_x = prepare_x(0, in_head=True)
+        for call in sets_w + sets_x:
+            call()
+        quantise_w()
+        quantise_x()
+        neg_sin_t = const.tile([P, NQ, J * NI], BF16)
+        nc.vector.tensor_scalar_mul(out=neg_sin_t[:], in0=sin_t[:], scalar1=-1.0)
+
+        chunks = {}
+        products_of = {}
+        group_sums = {}
+        v_sums = {}
+        waiting = {"reduces": []}
+
+        def store_chunk(span, t):
+            b, qt = divmod(span, NQ)
+            queue = nc.scalar if t == V_ else nc.sync
+            for g in range(GS):
                 queue.dma_start(
-                    out=outs[t][b, :, qt * GB + g, 0:P, :].rearrange("h (n j) c -> n h (j c)", j=J),
-                    in_=o[g:P:GB, :, :, :].rearrange("n h j c -> n h (j c)"),
+                    out=outs[t][b, :, qt * GS + g, 0:TG, :].rearrange("h (n j) c -> n h (j c)", j=J),
+                    in_=chunks[(span, t)][g:P:GS, :, :, :].rearrange("n h j c -> n h (j c)"),
                 )
 
-        o_of = {}
-        l1_of = {}
-        sums_of = {}
-        held = {"pending": []}
+        def rope_products(span, t, j):
+            qt = span % NQ
+            if (span, j // 2) not in products_of:
+                cos_prod = products.tile([P, 2 * H, 2, HS], F32, name="cos_prod")
+                sin_prod = products.tile([P, 2, 2 * H, 2, NI], F32, name="sin_prod")
+                products_of[(span, j // 2)] = (cos_prod, sin_prod)
+            cos_prod, sin_prod = products_of[(span, j // 2)]
+            heads = slice(t * H, (t + 1) * H)
+            angles = slice(j * NI, (j + 1) * NI)
+            bank = ps_pass.tile([P, C], F32, name="bank", tag="bank")
+            mx_pass(bank[:], span, j, t)
+            ab = bank[:].rearrange("p (h i x) -> p h i x", h=H, x=2)
+            nc.vector.tensor_tensor(
+                out=cos_prod[:, heads, j % 2, :].rearrange("p h (i x) -> p h i x", x=2),
+                in0=ab,
+                in1=cos_t[:, qt, angles].unsqueeze(1).unsqueeze(3).to_broadcast([P, H, NI, 2]),
+                op=MULT,
+            )
+            nc.vector.tensor_tensor(
+                out=sin_prod[:, 0, heads, j % 2, :],
+                in0=ab[:, :, :, 1],
+                in1=neg_sin_t[:, qt, angles].unsqueeze(1).to_broadcast([P, H, NI]),
+                op=MULT,
+            )
+            nc.vector.tensor_tensor(
+                out=sin_prod[:, 1, heads, j % 2, :],
+                in0=ab[:, :, :, 0],
+                in1=sin_t[:, qt, angles].unsqueeze(1).to_broadcast([P, H, NI]),
+                op=MULT,
+            )
 
-        def sums_qk(blk, t, half):
-            b, qt = divmod(blk, NQ)
-            o = o_of[(blk, t)]
-            st = ps_st.tile([P, 4, P], F32, name="st")
-            for hh in range(4):
-                if (blk, t) in l1_of:
-                    nc.tensor.transpose(out=st[:, hh, :], in_=l1_of[(blk, t)][:, 4 * half + hh, :], identity=ident[:])
-                else:
-                    for a in range(2):
-                        nc.tensor.matmul(
-                            out=st[:, hh, :],
-                            lhsT=o[:, 4 * half + hh, 2 * a : 2 * a + 2, :].rearrange("p j c -> p (j c)"),
-                            rhs=ident[:],
-                            is_transpose=True,
-                            start=(a == 0),
-                            stop=(a == 1),
-                        )
-            held["pending"].append(
+        def rope_add(span, t, slot_pair):
+            if slot_pair == 0:
+                chunk = chunk_pool.tile([P, H, J, HS], F32, name="chunk")
+                chunks[(span, t)] = chunk
+            cos_prod, sin_prod = products_of[(span, slot_pair)]
+            heads = slice(t * H, (t + 1) * H)
+            engine = nc.vector if (span, t) == (NSPAN - 1, K_) else nc.gpsimd
+            engine.tensor_tensor(
+                out=chunks[(span, t)][:, :, 2 * slot_pair : 2 * slot_pair + 2, :].rearrange("p h j (i x) -> p h (j i) x", x=2),
+                in0=cos_prod[:, heads, :, :].rearrange("p h j (i x) -> p h (j i) x", x=2),
+                in1=sin_prod[:, :, heads, :, :].rearrange("p x h j i -> p h (j i) x"),
+                op=ADD,
+            )
+            if slot_pair == 1:
+                store_chunk(span, t)
+
+        def v_slot(span, j):
+            b, qt = divmod(span, NQ)
+            if j == 0:
+                chunk = chunk_pool.tile([P, H, J, HS], F32, name="chunk")
+                chunks[(span, V_)] = chunk
+            bank = ps_pass.tile([P, C], F32, name="bank", tag="bank")
+            mx_pass(bank[:], span, j, V_)
+            nc.scalar.copy(out=chunks[(span, V_)][:, :, j, :], in_=bank[:].rearrange("p (h c) -> p h c", h=H))
+            if j == J - 1:
+                store_chunk(span, V_)
+            v_turned = ps_vt.tile([P, C], F32, name="v_turned")
+            two_heads = slice(V_ * C + j * P, V_ * C + (j + 1) * P)
+            positions = slice(span * C, (span + 1) * C)
+            nc.tensor.matmul_mx(
+                out=v_turned[:],
+                lhsT=w_codes[:, two_heads].bitcast(FP8X4),
+                lhsT_scale=w_scales[:, two_heads],
+                rhs=x_codes[:, positions].bitcast(FP8X4),
+                rhs_scale=x_scales[:, positions],
+                start=True,
+                stop=True,
+            )
+            by_group = v_turned[:].rearrange("m (j n g) -> m g j n", j=J, g=GS)
+            for g in range(GS):
+                unused = small.tile([P, J, P // GS], F32, name="unused")
+                nc.scalar.activation(
+                    out=unused[:],
+                    in_=by_group[:, g],
+                    func=COPY,
+                    accum_out=v_sums[b][:, j, qt * GS + g : qt * GS + g + 1],
+                )
+
+        def sum_tile(n):
+            span, t, first_head = n // SUM_TILES, (n % SUM_TILES) // 2, (n % 2) * HEADS_OF_TILE
+            b, qt = divmod(span, NQ)
+            turned = ps_sums.tile([P, HEADS_OF_TILE, P], F32, name="turned")
+            for h in range(HEADS_OF_TILE):
+                for slot_pair in range(2):
+                    nc.tensor.matmul(
+                        out=turned[:, h, :],
+                        lhsT=chunks[(span, t)][:, first_head + h, 2 * slot_pair : 2 * slot_pair + 2, :].rearrange("p j c -> p (j c)"),
+                        rhs=ident[:],
+                        is_transpose=True,
+                        start=(slot_pair == 0),
+                        stop=(slot_pair == 1),
+                    )
+            waiting["reduces"].append(
                 lambda: nc.vector.tensor_reduce(
-                    out=sums_of[b][:, t, 4 * half : 4 * half + 4, qt * GB : (qt + 1) * GB],
-                    in_=st[:].rearrange("m h (n g) -> m h g n", g=GB),
-                    axis=mybir.AxisListType.X,
+                    out=group_sums[b][:, t, first_head : first_head + HEADS_OF_TILE, qt * GS : (qt + 1) * GS],
+                    in_=turned[:].rearrange("m h (n g) -> m h g n", g=GS),
+                    axis=LAST_AXIS,
                     op=ADD,
                 )
             )
 
-        def flush_pending():
-            for item in held["pending"]:
-                item()
-            held["pending"] = []
+        def do_reduces():
+            for call in waiting["reduces"]:
+                call()
+            waiting["reduces"] = []
 
-        def means_out(b):
-            flush_pending()
-            rsb = sums_of[b]
+        def store_means(b):
+            do_reduces()
             nc.vector.tensor_tensor(
-                out=rsb[:, 2, :, :].rearrange("m (a x) g -> m a x g", x=2),
-                in0=sums_of[(b, "v")][:].unsqueeze(2).to_broadcast([P, 4, 2, G]),
-                in1=mask_v[:],
+                out=group_sums[b][:, V_, :, :].rearrange("m (a x) g -> m a x g", x=2),
+                in0=v_sums[b][:].unsqueeze(2).to_broadcast([P, H // 2, 2, G]),
+                in1=own_half[:],
                 op=MULT,
             )
-            mps = ps_tr.tile([P, 3 * HS], F32, name="tr")
+            means_ps = ps_words.tile([P, 3 * HS], F32, name="means_ps", tag="words")
             for t in range(3):
                 nc.tensor.matmul(
-                    out=mps[:, t * HS : (t + 1) * HS],
-                    lhsT=rsb[:, t, :, :].rearrange("m h g -> m (h g)"),
+                    out=means_ps[:, t * HS : (t + 1) * HS],
+                    lhsT=group_sums[b][:, t, :, :].rearrange("m h g -> m (h g)"),
                     rhs=fold[:],
                     start=True,
                     stop=True,
                 )
-            msb = small.tile([P, 3 * HS], F32, name="msb")
-            nc.scalar.copy(out=msb[:], in_=mps[:])
+            means = small.tile([P, 3 * HS], F32, name="means")
+            nc.scalar.copy(out=means[:], in_=means_ps[:])
             for t in range(3):
                 nc.sync.dma_start(
-                    out=outs[t][b, :, :, P, :].rearrange("h g c -> (h g) c"),
-                    in_=msb[:, t * HS : (t + 1) * HS],
+                    out=outs[t][b, :, :, TG, :].rearrange("h g c -> (h g) c"),
+                    in_=means[:, t * HS : (t + 1) * HS],
                 )
 
-        def final_add(engine, blk, t, jh):
-            o = o_of[(blk, t)]
-            k1, pl = held[(blk, jh)]
-            js = slice(2 * jh, 2 * jh + 2)
-            hs = slice(t * H, (t + 1) * H)
-            engine.tensor_tensor(
-                out=o[:, :, js, :].rearrange("p h j (i x) -> p h (j i) x", x=2),
-                in0=k1[:, hs, :, :].rearrange("p h j (i x) -> p h (j i) x", x=2),
-                in1=pl[:, :, hs, :, :].rearrange("p x h j i -> p h (j i) x"),
-                op=ADD,
-            )
-
-        def qk_unit(blk, t, j):
-            qt = blk % NQ
-            if (blk, j // 2) not in held:
-                k1 = work.tile([P, 2 * H, 2, HS], F32, name="k1")
-                pl = work.tile([P, 2, 2 * H, 2, NI], F32, name="pl")
-                held[(blk, j // 2)] = (k1, pl)
-            k1, pl = held[(blk, j // 2)]
-            hs = slice(t * H, (t + 1) * H)
-            js = slice(j * NI, (j + 1) * NI)
-            bank = ps_mm.tile([P, C], F32, name="mm")
-            mx_pass(bank[:], blk, j, t, True, True)
-            nc.vector.tensor_tensor(
-                out=k1[:, hs, j % 2, :].rearrange("p h (i x) -> p h i x", x=2),
-                in0=bank[:].rearrange("p (h i x) -> p h i x", h=H, x=2),
-                in1=cosb[:, qt, js].unsqueeze(1).unsqueeze(3).to_broadcast([P, H, NI, 2]),
-                op=MULT,
-            )
-            pairs = bank[:].rearrange("p (h i x) -> p h i x", h=H, x=2)
-            nc.vector.tensor_tensor(
-                out=pl[:, 0, hs, j % 2, :],
-                in0=pairs[:, :, :, 1],
-                in1=nsinb[:, qt, js].unsqueeze(1).to_broadcast([P, H, NI]),
-                op=MULT,
-            )
-            nc.vector.tensor_tensor(
-                out=pl[:, 1, hs, j % 2, :],
-                in0=pairs[:, :, :, 0],
-                in1=sinb[:, qt, js].unsqueeze(1).to_broadcast([P, H, NI]),
-                op=MULT,
-            )
-
-        def adds(blk, t, jh):
-            if jh == 0:
-                o = opool.tile([P, H, J, HS], F32, name="o")
-                o_of[(blk, t)] = o
-            on_vector = blk == NBLK - 1 and t == 1
-            final_add(nc.vector if on_vector else nc.gpsimd, blk, t, jh)
-            if jh == 1:
-                store_chunk(o_of[(blk, t)], blk, t)
-                if t == 1 and not on_vector:
-                    o = o_of[(blk, t)]
-                    l1 = lpool.tile([P, H, 2 * HS], F32, name="l1")
-                    nc.gpsimd.tensor_tensor(
-                        out=l1[:],
-                        in0=o[:, :, 0:2, :].rearrange("p h j c -> p h (j c)"),
-                        in1=o[:, :, 2:4, :].rearrange("p h j c -> p h (j c)"),
-                        op=ADD,
-                    )
-                    l1_of[(blk, t)] = l1
-
-        def v_pass(blk, j):
-            b, qt = divmod(blk, NQ)
-            if j == 0:
-                o = opool.tile([P, H, J, HS], F32, name="o")
-                held["ov"] = o
-            o = held["ov"]
-            vm = ps_mm.tile([P, C], F32, name="mm")
-            mx_pass(vm[:], blk, j, 2, True, True)
-            nc.scalar.copy(out=o[:, :, j, :], in_=vm[:].rearrange("p (h c) -> p h c", h=H))
-            if j == J - 1:
-                store_chunk(o, blk, 2)
-            vt = ps_va.tile([P, C], F32, name="vt")
-            wcol = 2 * C + j * P
-            nc.tensor.matmul_mx(
-                out=vt[:],
-                lhsT=wcodes[:, wcol : wcol + P].bitcast(FP8X4),
-                lhsT_scale=wscales[:, wcol : wcol + P],
-                rhs=xcodes[:, blk * C : (blk + 1) * C].bitcast(FP8X4),
-                rhs_scale=xscales[:, blk * C : (blk + 1) * C],
-                start=True,
-                stop=True,
-            )
-            by_group = vt[:].rearrange("m (j n g) -> m g j n", j=J, g=GB)
-            for g in range(GB):
-                junk = small.tile([P, J, P // GB], F32, name="junk")
-                nc.scalar.activation(
-                    out=junk[:],
-                    in_=by_group[:, g],
-                    func=mybir.ActivationFunctionType.Copy,
-                    accum_out=sums_of[(b, "v")][:, j, qt * GB + g : qt * GB + g + 1],
-                )
-
-        for blk in range(NBLK + 2):
-            if blk < NBLK and blk % NQ == 0:
-                rsb = small.tile([P, 3, H, G], F32, name="rsb")
-                rv = small.tile([P, 4, G], F32, name="rv")
-                sums_of[blk // NQ] = rsb
-                sums_of[(blk // NQ, "v")] = rv
-            slots = [[], [], [], []]
-            units = []
-            by_tensor = blk == 0 or blk == NBLK - 1
-            if blk < NBLK:
-                if by_tensor:
-                    order = [(t, j) for t in range(2) for j in range(J)]
+        first_w = {}
+        next_x = {}
+        for beat in range(NSPAN * BEATS + SUM_LAG):
+            span, s = divmod(beat, BEATS)
+            side = []
+            if span < NSPAN:
+                if s == 0 and span % NQ == 0:
+                    sums_qkv = small.tile([P, 3, H, G], F32, name="sums_qkv")
+                    sums_v = small.tile([P, H // 2, G], F32, name="sums_v")
+                    group_sums[span // NQ] = sums_qkv
+                    v_sums[span // NQ] = sums_v
+                tensor_by_tensor = span == 0 or span == NSPAN - 1
+                if tensor_by_tensor:
+                    passes = [(s // 2, 2 * (s % 2)), (s // 2, 2 * (s % 2) + 1)]
+                    due = [(s // 2, s % 2)]
                 else:
-                    order = [(t, j) for j in range(J) for t in range(2)]
-                units = [order[0:2], order[2:4], order[4:6], order[6:8]]
-                vp = [lambda j=j: v_pass(blk, j) for j in range(J)]
-                if blk == 0:
-                    trs_k, quantise_k = prep_w(1)
-                    trs_v, quantise_v = prep_w(2)
-                    trs, quantise = prep_x(1)
-                    slots[0] += trs_k
-                    slots[1] += [quantise_k] + trs_v
-                    slots[2] += [quantise_v] + trs + [vp[0], vp[1]]
-                    slots[3] += [quantise, vp[2], vp[3]]
+                    passes = [(Q_, s), (K_, s)]
+                    due = [(Q_, s // 2), (K_, s // 2)] if s % 2 == 1 else []
+                if beat == 0:
+                    first_w[K_] = prepare_w(K_)
+                    first_w[V_] = prepare_w(V_)
+                if s == 0 and span + 1 < NSPAN:
+                    next_x["sets"], next_x["quantise"] = prepare_x(span + 1)
+                if span == 0:
+                    if s == 0:
+                        side += first_w[K_][0]
+                    elif s == 1:
+                        side += [first_w[K_][1]] + first_w[V_][0]
+                    elif s == 2:
+                        side += [first_w[V_][1]] + next_x["sets"] + [lambda: v_slot(0, 0), lambda: v_slot(0, 1)]
+                    else:
+                        side += [next_x["quantise"], lambda: v_slot(0, 2), lambda: v_slot(0, 3)]
                 else:
-                    for j in range(J):
-                        slots[j].append(vp[j])
-                    if blk + 1 < NBLK:
-                        trs, quantise = prep_x(blk + 1)
-                        slots[0] += trs[0:2]
-                        slots[1] += trs[2:4]
-                        slots[2] += [quantise]
-            for s in range(4):
-                tile_nos = [blk * 4 + s - SUM_LAG]
-                if blk * 4 + s > (NBLK - 1) * 4:
-                    tile_nos = [blk * 4 + s - SUM_LAG + 1]
-                    if blk * 4 + s == (NBLK - 1) * 4 + 1:
-                        tile_nos = [blk * 4 + s - SUM_LAG, blk * 4 + s - SUM_LAG + 1]
-                for tile_no in tile_nos:
-                    if 0 <= tile_no < NBLK * 4:
-                        slots[s].append(lambda n=tile_no: sums_qk(n // 4, (n % 4) // 2, n % 2))
-                        if tile_no % (NQ * 4) == NQ * 4 - 1:
-                            slots[s].append(lambda n=tile_no: means_out(n // (NQ * 4)))
-            for s in range(4):
-                if blk < NBLK:
-                    for t, j in units[s]:
-                        qk_unit(blk, t, j)
-                flush_pending()
-                if blk < NBLK:
-                    if by_tensor:
-                        adds(blk, s // 2, s % 2)
-                    elif s % 2 == 1:
-                        adds(blk, 0, s // 2)
-                        adds(blk, 1, s // 2)
-                for item in slots[s]:
-                    item()
+                    side.append(lambda: v_slot(span, s))
+                    if span + 1 < NSPAN:
+                        if s < 2:
+                            side += next_x["sets"][2 * s : 2 * s + 2]
+                        elif s == 2:
+                            side.append(next_x["quantise"])
+            n = beat - SUM_LAG
+            if n >= 0:
+                side.append(lambda: sum_tile(n))
+                if n % (NQ * SUM_TILES) == NQ * SUM_TILES - 1:
+                    side.append(lambda: store_means(n // (NQ * SUM_TILES)))
+
+            if span < NSPAN:
+                for t, j in passes:
+                    rope_products(span, t, j)
+            do_reduces()
+            if span < NSPAN:
+                for t, slot_pair in due:
+                    rope_add(span, t, slot_pair)
+            for call in side:
+                call()

from contextlib import ExitStack

import concourse.mybir as mybir
from concourse.masks import make_identity

F32 = mybir.dt.float32
BF16 = mybir.dt.bfloat16
U32 = mybir.dt.uint32
U8 = mybir.dt.uint8
FP8X4 = mybir.dt.float8_e4m3fn_x4
ADD = mybir.AluOpType.add
MULT = mybir.AluOpType.mult
COPY = mybir.ActivationFunctionType.Copy
LAST_AXIS = mybir.AxisListType.X

P = 128
B, T, C, H, G = 2, 2048, 512, 8, 16
HS = C // H
NI = HS // 2
TG = T // G
J = 4
GS = P * J // TG
NQ = T // (P * J)
NSPAN = B * NQ
WORDS = C // 2
PLANES = WORDS // P
PACK = 4
SETS = 4
HEADS_OF_TILE = 4
Q_, K_, V_ = 0, 1, 2
BEATS = 4
SUM_TILES = 4
SUM_LAG = 5
FLOPS = 2 * B * T * 3 * C * C


def tile_causalselfattention2_pa_t_kernel(tc, x, w_attn, freqs_cos, freqs_sin, out_0, out_1, out_2):
    nc = tc.nc
    outs = [out_0, out_1, out_2]
    with ExitStack() as ctx:
        const = ctx.enter_context(tc.tile_pool(name="const", bufs=1))
        x_pool = ctx.enter_context(tc.tile_pool(name="x_pool", bufs=NSPAN))
        stage = ctx.enter_context(tc.tile_pool(name="stage", bufs=2))
        products = ctx.enter_context(tc.tile_pool(name="products", bufs=4))
        chunk_pool = ctx.enter_context(tc.tile_pool(name="chunk_pool", bufs=7))
        small = ctx.enter_context(tc.tile_pool(name="small", bufs=2))
        ps_words = ctx.enter_context(tc.psum_pool(name="ps_words", bufs=1))
        ps_pass = ctx.enter_context(tc.psum_pool(name="ps_pass", bufs=4))
        ps_vt = ctx.enter_context(tc.psum_pool(name="ps_vt", bufs=1))
        ps_sums = ctx.enter_context(tc.psum_pool(name="ps_sums", bufs=2))
        ctx.enter_context(tc.manual_schedule())

        w_rows = const.tile([P, 3 * SETS, C], BF16)
        w_view = w_attn.rearrange("(r p) k -> p r k", p=P)
        x_rows = []
        for span in range(NSPAN):
            x_span = x_pool.tile([P, J * C], BF16, name="x_span")
            x_rows.append(x_span)

        def load_w(t):
            nc.sync.dma_start(out=w_rows[:, SETS * t : SETS * (t + 1), :], in_=w_view[:, SETS * t : SETS * (t + 1), :])

        def load_x(span):
            b, qt = divmod(span, NQ)
            nc.sync.dma_start(
                out=x_rows[span][:],
                in_=x[b, qt * P * J : (qt + 1) * P * J, :].rearrange("(p j) k -> p (j k)", j=J),
            )

        load_w(Q_)
        load_x(0)
        load_w(K_)
        load_w(V_)
        for span in range(1, NSPAN):
            load_x(span)

        cos_t = const.tile([P, NQ, J * NI], BF16)
        sin_t = const.tile([P, NQ, J * NI], BF16)
        cos_view = freqs_cos.rearrange("(q g n j) i -> g n q (j i)", q=NQ, g=GS, j=J)
        sin_view = freqs_sin.rearrange("(q g n j) i -> g n q (j i)", q=NQ, g=GS, j=J)
        for g in range(GS):
            nc.scalar.dma_start(out=cos_t[g:P:GS, :, :], in_=cos_view[g])
            nc.scalar.dma_start(out=sin_t[g:P:GS, :, :], in_=sin_view[g])

        ident = const.tile([P, P], F32)
        make_identity(nc, ident[:])
        spread = const.tile([P, P], F32)
        nc.vector.tensor_copy(
            out=spread[:].rearrange("k (n g) -> k n g", g=GS),
            in_=ident[:].rearrange("k (g n) -> k n g", g=GS),
        )
        fold = const.tile([P, HS], F32)
        nc.vector.tensor_tensor(out=fold[:], in0=ident[:, 0:HS], in1=ident[:, HS:P], op=ADD)
        nc.vector.tensor_scalar_mul(out=fold[:], in0=fold[:], scalar1=1.0 / TG)
        own_half = const.tile([P, H // 2, 2, G], F32)
        nc.vector.memset(own_half[:], 1.0)
        nc.vector.memset(own_half[0:HS, :, 1, :], 0.0)
        nc.vector.memset(own_half[HS:P, :, 0, :], 0.0)

        w_codes = const.tile([P, 3 * C], U32, align_bytes=64)
        w_scales = const.tile([P, 3 * C], U8, align_bytes=64)
        x_codes = const.tile([P, NSPAN * C], U32, align_bytes=64)
        x_scales = const.tile([P, NSPAN * C], U8, align_bytes=64)
        w_words = w_rows[:].bitcast(F32)

        def prepare(words, matrix, columns, codes, scales, in_head, copy):
            grouped = stage.tile([P, SETS * P * PACK], BF16, align_bytes=64, name="grouped")
            grouped_words = grouped[:].bitcast(F32).rearrange("q (s m u) -> q s m u", s=SETS, u=PLANES)
            current = {}

            def transpose_set(s):
                if s % 2 == 0:
                    if in_head:
                        planes = ps_pass.tile([P, 2, PLANES, P], F32, name="planes", tag="bank")
                    else:
                        planes = ps_words.tile([P, 2, PLANES, P], F32, name="planes", tag="words")
                    current["planes"] = planes
                planes = current["planes"]
                for u in range(PLANES):
                    nc.tensor.transpose(out=planes[:, s % 2, u, :], in_=words(s, u), identity=matrix[:])
                if s % 2 == 1:
                    copy(out=grouped_words[:, s - 1 : s + 1], in_=planes[:].rearrange("q s u m -> q s m u"))

            def quantise():
                nc.vector.quantize_mx(out=codes[:, columns].bitcast(FP8X4), scales=scales[:, columns], in_=grouped[:])

            return [lambda s=s: transpose_set(s) for s in range(SETS)], quantise

        def prepare_w(t, in_head=False):
            return prepare(
                lambda s, u: w_words[:, SETS * t + s, u * P : (u + 1) * P],
                ident,
                slice(t * C, (t + 1) * C),
                w_codes,
                w_scales,
                in_head,
                nc.scalar.copy,
            )

        def prepare_x(span, in_head=False):
            x_words = x_rows[span][:].bitcast(F32)
            return prepare(
                lambda s, u: x_words[:, s * WORDS + u * P : s * WORDS + (u + 1) * P],
                spread,
                slice(span * C, (span + 1) * C),
                x_codes,
                x_scales,
                in_head,
                nc.vector.tensor_copy if in_head else nc.scalar.copy,
            )

        def mx_pass(out, span, j, t):
            positions = slice((span * J + j) * P, (span * J + j + 1) * P)
            channels = slice(t * C, (t + 1) * C)
            nc.tensor.matmul_mx(
                out=out,
                lhsT=x_codes[:, positions].bitcast(FP8X4),
                lhsT_scale=x_scales[:, positions],
                rhs=w_codes[:, channels].bitcast(FP8X4),
                rhs_scale=w_scales[:, channels],
                start=True,
                stop=True,
            )

        sets_w, quantise_w = prepare_w(Q_, in_head=True)
        sets_x, quantise_x = prepare_x(0, in_head=True)
        for call in sets_w + sets_x:
            call()
        quantise_w()
        quantise_x()
        neg_sin_t = const.tile([P, NQ, J * NI], BF16)
        nc.vector.tensor_scalar_mul(out=neg_sin_t[:], in0=sin_t[:], scalar1=-1.0)

        chunks = {}
        products_of = {}
        group_sums = {}
        v_sums = {}
        waiting = {"reduces": []}

        def store_chunk(span, t):
            b, qt = divmod(span, NQ)
            queue = nc.scalar if t == V_ else nc.sync
            for g in range(GS):
                queue.dma_start(
                    out=outs[t][b, :, qt * GS + g, 0:TG, :].rearrange("h (n j) c -> n h (j c)", j=J),
                    in_=chunks[(span, t)][g:P:GS, :, :, :].rearrange("n h j c -> n h (j c)"),
                )

        def rope_products(span, t, j):
            qt = span % NQ
            if (span, j // 2) not in products_of:
                cos_prod = products.tile([P, 2 * H, 2, HS], F32, name="cos_prod")
                sin_prod = products.tile([P, 2, 2 * H, 2, NI], F32, name="sin_prod")
                products_of[(span, j // 2)] = (cos_prod, sin_prod)
            cos_prod, sin_prod = products_of[(span, j // 2)]
            heads = slice(t * H, (t + 1) * H)
            angles = slice(j * NI, (j + 1) * NI)
            bank = ps_pass.tile([P, C], F32, name="bank", tag="bank")
            mx_pass(bank[:], span, j, t)
            ab = bank[:].rearrange("p (h i x) -> p h i x", h=H, x=2)
            nc.vector.tensor_tensor(
                out=cos_prod[:, heads, j % 2, :].rearrange("p h (i x) -> p h i x", x=2),
                in0=ab,
                in1=cos_t[:, qt, angles].unsqueeze(1).unsqueeze(3).to_broadcast([P, H, NI, 2]),
                op=MULT,
            )
            nc.vector.tensor_tensor(
                out=sin_prod[:, 0, heads, j % 2, :],
                in0=ab[:, :, :, 1],
                in1=neg_sin_t[:, qt, angles].unsqueeze(1).to_broadcast([P, H, NI]),
                op=MULT,
            )
            nc.vector.tensor_tensor(
                out=sin_prod[:, 1, heads, j % 2, :],
                in0=ab[:, :, :, 0],
                in1=sin_t[:, qt, angles].unsqueeze(1).to_broadcast([P, H, NI]),
                op=MULT,
            )

        def rope_add(span, t, slot_pair):
            if slot_pair == 0:
                chunk = chunk_pool.tile([P, H, J, HS], F32, name="chunk")
                chunks[(span, t)] = chunk
            cos_prod, sin_prod = products_of[(span, slot_pair)]
            heads = slice(t * H, (t + 1) * H)
            engine = nc.vector if (span, t) == (NSPAN - 1, K_) else nc.gpsimd
            engine.tensor_tensor(
                out=chunks[(span, t)][:, :, 2 * slot_pair : 2 * slot_pair + 2, :].rearrange("p h j (i x) -> p h (j i) x", x=2),
                in0=cos_prod[:, heads, :, :].rearrange("p h j (i x) -> p h (j i) x", x=2),
                in1=sin_prod[:, :, heads, :, :].rearrange("p x h j i -> p h (j i) x"),
                op=ADD,
            )
            if slot_pair == 1:
                store_chunk(span, t)

        def v_slot(span, j):
            b, qt = divmod(span, NQ)
            if j == 0:
                chunk = chunk_pool.tile([P, H, J, HS], F32, name="chunk")
                chunks[(span, V_)] = chunk
            bank = ps_pass.tile([P, C], F32, name="bank", tag="bank")
            mx_pass(bank[:], span, j, V_)
            nc.scalar.copy(out=chunks[(span, V_)][:, :, j, :], in_=bank[:].rearrange("p (h c) -> p h c", h=H))
            if j == J - 1:
                store_chunk(span, V_)
            v_turned = ps_vt.tile([P, C], F32, name="v_turned")
            two_heads = slice(V_ * C + j * P, V_ * C + (j + 1) * P)
            positions = slice(span * C, (span + 1) * C)
            nc.tensor.matmul_mx(
                out=v_turned[:],
                lhsT=w_codes[:, two_heads].bitcast(FP8X4),
                lhsT_scale=w_scales[:, two_heads],
                rhs=x_codes[:, positions].bitcast(FP8X4),
                rhs_scale=x_scales[:, positions],
                start=True,
                stop=True,
            )
            by_group = v_turned[:].rearrange("m (j n g) -> m g j n", j=J, g=GS)
            for g in range(GS):
                unused = small.tile([P, J, P // GS], F32, name="unused")
                nc.scalar.activation(
                    out=unused[:],
                    in_=by_group[:, g],
                    func=COPY,
                    accum_out=v_sums[b][:, j, qt * GS + g : qt * GS + g + 1],
                )

        def sum_tile(n):
            span, t, first_head = n // SUM_TILES, (n % SUM_TILES) // 2, (n % 2) * HEADS_OF_TILE
            b, qt = divmod(span, NQ)
            turned = ps_sums.tile([P, HEADS_OF_TILE, P], F32, name="turned")
            for h in range(HEADS_OF_TILE):
                for slot_pair in range(2):
                    nc.tensor.matmul(
                        out=turned[:, h, :],
                        lhsT=chunks[(span, t)][:, first_head + h, 2 * slot_pair : 2 * slot_pair + 2, :].rearrange("p j c -> p (j c)"),
                        rhs=ident[:],
                        is_transpose=True,
                        start=(slot_pair == 0),
                        stop=(slot_pair == 1),
                    )
            waiting["reduces"].append(
                lambda: nc.vector.tensor_reduce(
                    out=group_sums[b][:, t, first_head : first_head + HEADS_OF_TILE, qt * GS : (qt + 1) * GS],
                    in_=turned[:].rearrange("m h (n g) -> m h g n", g=GS),
                    axis=LAST_AXIS,
                    op=ADD,
                )
            )

        def do_reduces():
            for call in waiting["reduces"]:
                call()
            waiting["reduces"] = []

        def store_means(b):
            do_reduces()
            nc.vector.tensor_tensor(
                out=group_sums[b][:, V_, :, :].rearrange("m (a x) g -> m a x g", x=2),
                in0=v_sums[b][:].unsqueeze(2).to_broadcast([P, H // 2, 2, G]),
                in1=own_half[:],
                op=MULT,
            )
            means_ps = ps_words.tile([P, 3 * HS], F32, name="means_ps", tag="words")
            for t in range(3):
                nc.tensor.matmul(
                    out=means_ps[:, t * HS : (t + 1) * HS],
                    lhsT=group_sums[b][:, t, :, :].rearrange("m h g -> m (h g)"),
                    rhs=fold[:],
                    start=True,
                    stop=True,
                )
            means = small.tile([P, 3 * HS], F32, name="means")
            nc.scalar.copy(out=means[:], in_=means_ps[:])
            for t in range(3):
                nc.sync.dma_start(
                    out=outs[t][b, :, :, TG, :].rearrange("h g c -> (h g) c"),
                    in_=means[:, t * HS : (t + 1) * HS],
                )

        first_w = {}
        next_x = {}
        for beat in range(NSPAN * BEATS + SUM_LAG):
            span, s = divmod(beat, BEATS)
            side = []
            if span < NSPAN:
                if s == 0 and span % NQ == 0:
                    sums_qkv = small.tile([P, 3, H, G], F32, name="sums_qkv")
                    sums_v = small.tile([P, H // 2, G], F32, name="sums_v")
                    group_sums[span // NQ] = sums_qkv
                    v_sums[span // NQ] = sums_v
                tensor_by_tensor = span == 0 or span == NSPAN - 1
                if tensor_by_tensor:
                    passes = [(s // 2, 2 * (s % 2)), (s // 2, 2 * (s % 2) + 1)]
                    due = [(s // 2, s % 2)]
                else:
                    passes = [(Q_, s), (K_, s)]
                    due = [(Q_, s // 2), (K_, s // 2)] if s % 2 == 1 else []
                if beat == 0:
                    first_w[K_] = prepare_w(K_)
                    first_w[V_] = prepare_w(V_)
                if s == 0 and span + 1 < NSPAN:
                    next_x["sets"], next_x["quantise"] = prepare_x(span + 1)
                if span == 0:
                    if s == 0:
                        side += first_w[K_][0]
                    elif s == 1:
                        side += [first_w[K_][1]] + first_w[V_][0]
                    elif s == 2:
                        side += [first_w[V_][1]] + next_x["sets"] + [lambda: v_slot(0, 0), lambda: v_slot(0, 1)]
                    else:
                        side += [next_x["quantise"], lambda: v_slot(0, 2), lambda: v_slot(0, 3)]
                else:
                    side.append(lambda: v_slot(span, s))
                    if span + 1 < NSPAN:
                        if s < 2:
                            side += next_x["sets"][2 * s : 2 * s + 2]
                        elif s == 2:
                            side.append(next_x["quantise"])
            n = beat - SUM_LAG
            if n >= 0:
                side.append(lambda: sum_tile(n))
                if n % (NQ * SUM_TILES) == NQ * SUM_TILES - 1:
                    side.append(lambda: store_means(n // (NQ * SUM_TILES)))

            if span < NSPAN:
                for t, j in passes:
                    rope_products(span, t, j)
            do_reduces()
            if span < NSPAN:
                for t, slot_pair in due:
                    rope_add(span, t, slot_pair)
            for call in side:
                call()
